import numpy as np
import ml_dtypes


def mxq(x, axis, fmt="e4m3"):
    dtype, down = {"e4m3": (ml_dtypes.float8_e4m3fn, 7), "e5m2": (ml_dtypes.float8_e5m2, 14)}[fmt]
    v = np.moveaxis(np.asarray(x, np.float32).astype(ml_dtypes.bfloat16).astype(np.float64), axis, -1)
    blocks = v.reshape(v.shape[:-1] + (-1, 32))
    amax = np.abs(blocks).max(-1, keepdims=True)
    byte = np.maximum(np.where(amax > 0, np.frexp(amax)[1] - 1 + 127, 0) - down, 1)
    scale = np.exp2(byte - 127.0)
    codes = (blocks / scale).astype(np.float32).astype(dtype).astype(np.float64)
    return np.moveaxis((codes * scale).reshape(v.shape), -1, axis)


WIDE = False


def mx_kscale(k):
    if not WIDE:
        return np.ones(k)
    levels = np.array([10, -10, 5, -5, 0])
    if k % 512:
        return np.exp2(np.random.permutation(np.resize(levels, k // 32))).repeat(32)
    a = np.empty((k // 512, 16))
    for p in range(k // 512):
        a[p, :8] = np.random.permutation(np.resize(levels, 8))
        for g in range(8):
            far = levels[np.abs(levels - a[p, g]) >= 10]
            a[p, g + 8] = far[np.random.randint(len(far))]
    return np.exp2(a.ravel()).repeat(32)


BF16 = ml_dtypes.bfloat16


def bf(x):
    return np.asarray(x, np.float32).astype(BF16)


def f64(x):
    return np.asarray(x).astype(np.float64)


B, S, E, LAT, H = 4, 512, 8192, 2048, 64
D = E // H
R = D // 2
HR = H * R


def rope_cos_sin(n):
    inv_freq = 1.0 / (10000.0 ** (np.arange(0, R, 2) / R))
    freqs = np.outer(np.arange(n), inv_freq)
    emb = np.concatenate([freqs, freqs], axis=-1)
    return np.cos(emb), np.sin(emb)


def rotate_half(v):
    v1, v2 = v[..., : R // 2], v[..., R // 2 :]
    return np.concatenate([-v2, v1], axis=-1)


def apply_rope(v, cos, sin):
    return v * cos[None, :, None, :] + rotate_half(v) * sin[None, :, None, :]


def setup_inputs():
    s, t = mx_kscale(E), mx_kscale(LAT)
    return {
        "x": bf(np.random.standard_normal((B, S, E)) * s),
        "Wq_d": bf(np.random.standard_normal((LAT, E)) / np.sqrt(E) * t[:, None] / s[None, :]),
        "bq_d": bf(np.random.standard_normal(LAT) * 0.3 * t),
        "Wq_u": bf(np.random.standard_normal((HR, LAT)) / np.sqrt(LAT) / t[None, :]),
        "bq_u": bf(np.random.standard_normal(HR) * 0.3),
        "Wrq": bf(np.random.standard_normal((HR, LAT)) / np.sqrt(LAT) / t[None, :]),
        "brq": bf(np.random.standard_normal(HR) * 0.3),
    }


def reference(x, Wq_d, bq_d, Wq_u, bq_u, Wrq, brq):
    q_d = (mxq(f64(x), 2, "e4m3") @ mxq(f64(Wq_d), 1, "e4m3").T) + f64(bq_d)
    qdq = mxq(q_d, 2, "e4m3")
    q1 = ((qdq @ mxq(f64(Wq_u), 1, "e4m3").T) + f64(bq_u)).reshape(B, S, H, R)
    qr = ((qdq @ mxq(f64(Wrq), 1, "e4m3").T) + f64(brq)).reshape(B, S, H, R)
    cos, sin = rope_cos_sin(S)
    qr = apply_rope(qr, cos, sin)
    return np.concatenate([q1, qr], axis=-1)

@@ -1,0 +1,448 @@
+from contextlib import ExitStack
+
+import concourse.mybir as mybir
+from concourse.masks import make_identity
+
+FLOPS = 2 * 2048 * 8192 * 2048 * 2
+
+F32 = mybir.dt.float32
+BF16 = mybir.dt.bfloat16
+U32 = mybir.dt.uint32
+I32 = mybir.dt.int32
+U8 = mybir.dt.uint8
+FP8X4 = mybir.dt.float8_e4m3fn_x4
+ALU = mybir.AluOpType
+ACT = mybir.ActivationFunctionType
+
+P = 128
+PI = 3.141592653589793
+NSLOT = 25
+USE_G = True
+LD_HEAD = 3
+LD_STEADY = 2
+QLAG = 1
+KH = 3
+MAXP = 8
+LAG = 2
+
+
+def tile_multiheadlatentattention_pa_l_kernel(tc, x, Wq_d, bq_d, Wq_u, bq_u, Wrq, brq, out):
+    nc = tc.nc
+    x_flat = x.flatten_outer_dims()
+    out_flat = out.rearrange("b s h d -> (b s) (h d)")
+    wd_view = Wq_d.rearrange("(g m t) k -> g t m k", g=4, t=4)
+
+    with ExitStack() as ctx:
+        ctx.enter_context(tc.manual_schedule())
+        sb = ctx.enter_context(tc.tile_pool(name="sb", bufs=1))
+        ps = ctx.enter_context(tc.psum_pool(name="ps", bufs=4))
+
+        def slot(shape, dtype, name):
+            return sb.tile(shape, dtype, name=name, tag="slot", bufs=NSLOT, align_bytes=64)
+
+        ident = sb.tile([P, P], F32, name="ident")
+        make_identity(nc, ident[:])
+        bqd_sb = sb.tile([P, 16], BF16, name="bqd_sb")
+        trig = sb.tile([P, 512], F32, name="trig")
+        qp = sb.tile([P, 2048], U8, name="qp", align_bytes=64)
+
+        runs = []
+        for hf in (0, 1):
+            runs.append(("wd", 0, hf))
+            for rt in range(4):
+                runs.append(("x", rt, hf))
+            for grp in range(1, KH):
+                runs.append(("wd", grp, hf))
+        for c in (1, 2, 3):
+            for hf in (0, 1):
+                for rt in range(4):
+                    runs.append(("x", 4 * c + rt, hf))
+        NHEAD = len(runs)
+        for grp in range(KH, 16):
+            for hf in (0, 1):
+                runs.append(("wd", grp, hf))
+        for unit in range(16):
+            for rp in (0, 1):
+                runs.append(("w2", unit, rp))
+        NRUN = len(runs)
+
+        raw = {}
+        srt = {}
+        tps = {}
+        grpd = {}
+        wc = {}
+        wp = {}
+        uc = {}
+        up = {}
+        xc = {}
+        xp = {}
+        qc = {}
+        qg = {}
+
+        def load(i):
+            kind, a, b = runs[i]
+            r = slot([P, 4096], BF16, "raw")
+            raw[i] = r
+            if kind == "x":
+                nc.sync.dma_start(out=r[:], in_=x_flat[a * P:(a + 1) * P, b * 4096:(b + 1) * 4096])
+            elif kind == "wd":
+                nc.sync.dma_start(out=r[:], in_=wd_view[a // 4, a % 4][:, b * 4096:(b + 1) * 4096])
+            else:
+                w = Wq_u if a % 2 == 0 else Wrq
+                r0 = (a // 2) * 512 + b * 256
+                nc.sync.dma_start(
+                    out=r[:].rearrange("p (r k) -> p r k", r=2),
+                    in_=w[r0:r0 + 256, :].rearrange("(r p) k -> p r k", p=P),
+                )
+
+        def sort(i, on_scalar):
+            s = slot([P, 2048], F32, "srt")
+            srt[i] = s
+            dst = s[:].rearrange("p (b u q) -> p b u q", b=8, u=2)
+            src = raw[i][:].bitcast(F32).rearrange("p (b q u) -> p b u q", b=8, u=2)
+            if on_scalar:
+                nc.scalar.copy(out=dst, in_=src)
+            else:
+                nc.vector.tensor_copy(out=dst, in_=src)
+
+        def transp(i):
+            banks = []
+            for k in range(4):
+                t = ps.tile([P, 4, P], F32, name="tp", tag="tp", bufs=4)
+                banks.append(t)
+                for s in range(4):
+                    c0 = (k * 4 + s) * P
+                    nc.tensor.transpose(out=t[:, s, :], in_=srt[i][:, c0:c0 + P], identity=ident[:])
+            tps[i] = banks
+
+        def copyout(i):
+            g = slot([P, 4096], BF16, "grpd")
+            grpd[i] = g
+            gw = g[:].bitcast(F32)
+            for k in range(4):
+                nc.scalar.copy(
+                    out=gw[:, k * 512:(k + 1) * 512].rearrange("p (b r u) -> p b r u", b=2, u=2),
+                    in_=tps[i][k][:].rearrange("p (b u) r -> p b r u", u=2),
+                )
+
+        def quant(i):
+            kind, a, b = runs[i]
+            g = grpd[i]
+            if kind == "wd":
+                if b == 0:
+                    wc[a] = slot([P, 2048], U32, "wc")
+                    wp[a] = sb.tile([P, 512], U8, name="wp", tag="wp", bufs=4, align_bytes=64)
+                for j2 in (0, 1):
+                    j = b * 2 + j2
+                    nc.vector.quantize_mx(
+                        out=wc[a][:, j * 512:(j + 1) * 512].bitcast(FP8X4),
+                        scales=wp[a][4 * j:P, :],
+                        in_=g[:, j2 * 2048:(j2 + 1) * 2048],
+                    )
+            elif kind == "x":
+                c, rt = a // 4, a % 4
+                if rt == 0 and b == 0:
+                    xp[c] = sb.tile([P, 2048], U8, name="xp", tag="xp", bufs=4, align_bytes=64)
+                for blk in range(8):
+                    gp = b * 8 + blk
+                    j = gp // 4
+                    if rt == 0 and gp % 4 == 0:
+                        xc[(c, j)] = slot([P, 2048], U32, "xc")
+                    c0 = (gp % 4) * 512 + rt * P
+                    nc.vector.quantize_mx(
+                        out=xc[(c, j)][:, c0:c0 + P].bitcast(FP8X4),
+                        scales=xp[c][4 * j:P, c0:c0 + P],
+                        in_=g[:, blk * 512:(blk + 1) * 512],
+                    )
+            else:
+                if b == 0:
+                    uc[a] = slot([P, 2048], U32, "uc")
+                    up[a] = sb.tile([P, 512], U8, name="up", tag="wp", bufs=4, align_bytes=64)
+                for blk in range(8):
+                    r, gl = blk // 4, blk % 4
+                    c0 = (b * 2 + r) * P
+                    nc.vector.quantize_mx(
+                        out=uc[a][:, gl * 512 + c0:gl * 512 + c0 + P].bitcast(FP8X4),
+                        scales=up[a][4 * gl:P, c0:c0 + P],
+                        in_=g[:, blk * 512:(blk + 1) * 512],
+                    )
+
+        acc1 = {}
+
+        def mm1(grp, c, g0, g1):
+            if g0 == 0:
+                acc1[(grp, c)] = ps.tile([P, 512], F32, name="acc", tag="acc", bufs=4)
+            a = acc1[(grp, c)]
+            for gp in range(g0, g1):
+                j = gp // 4
+                nc.tensor.matmul_mx(
+                    out=a[:],
+                    lhsT=wc[grp][:, gp * P:(gp + 1) * P].bitcast(FP8X4),
+                    lhsT_scale=wp[grp][4 * j:P, (gp % 4) * P:(gp % 4 + 1) * P],
+                    rhs=xc[(c, j)][:, (gp % 4) * 512:(gp % 4 + 1) * 512].bitcast(FP8X4),
+                    rhs_scale=xp[c][4 * j:P, (gp % 4) * 512:(gp % 4 + 1) * 512],
+                    start=(gp == 0),
+                    stop=(gp == 15),
+                )
+
+        def evac1(grp, c):
+            gl, t = grp // 4, grp % 4
+            if t == 0:
+                qg[c] = sb.tile([P, 2048], BF16, name="qg", tag="qg", bufs=4, align_bytes=64)
+            nc.scalar.activation(
+                out=qg[c][:].rearrange("p (n t) -> p n t", t=4)[:, :, t],
+                in_=acc1[(grp, c)][:],
+                func=ACT.Identity,
+                bias=bqd_sb[:, grp:grp + 1],
+                scale=1.0,
+            )
+
+        def quant_q(gl, c):
+            if c == 0:
+                qc[gl] = slot([P, 2048], U32, "qc")
+            nc.vector.quantize_mx(
+                out=qc[gl][:, c * 512:(c + 1) * 512].bitcast(FP8X4),
+                scales=qp[4 * gl:P, c * 512:(c + 1) * 512],
+                in_=qg[c][:],
+            )
+
+        acc2 = {}
+        bias2 = {}
+        tuv = {}
+        otile = {}
+
+        def mm2(hc, tt):
+            for which in (1, 0):
+                a = ps.tile([P, 512], F32, name="acc", tag="acc", bufs=4)
+                acc2[(hc, tt, which)] = a
+                u = hc * 2 + which
+                for gl in range(4):
+                    nc.tensor.matmul_mx(
+                        out=a[:],
+                        lhsT=qc[gl][:, tt * P:(tt + 1) * P].bitcast(FP8X4),
+                        lhsT_scale=qp[4 * gl:P, tt * P:(tt + 1) * P],
+                        rhs=uc[u][:, gl * 512:(gl + 1) * 512].bitcast(FP8X4),
+                        rhs_scale=up[u][4 * gl:P, :],
+                        start=(gl == 0),
+                        stop=(gl == 3),
+                    )
+
+        def epi_a(hc, tt):
+            o = slot([P, 1024], F32, "o")
+            otile[(hc, tt)] = o
+            o3 = o[:].rearrange("p (h d) -> p h d", h=8)
+            w = slot([P, 1536], F32, "tuv")
+            tuv[(hc, tt)] = w
+            nc.vector.tensor_tensor(
+                out=w[:, 0:512],
+                in0=acc2[(hc, tt, 1)][:],
+                in1=bias2[1][:, hc * 512:(hc + 1) * 512],
+                op=ALU.add,
+            )
+            nc.vector.tensor_tensor(
+                out=o3[:, :, 0:64],
+                in0=acc2[(hc, tt, 0)][:].rearrange("p (h d) -> p h d", h=8),
+                in1=bias2[0][:, hc * 512:(hc + 1) * 512].rearrange("p (h d) -> p h d", h=8),
+                op=ALU.add,
+            )
+
+        def epi_b(hc, tt):
+            a = tt % 4
+            w = tuv[(hc, tt)]
+            t3 = w[:, 0:512].rearrange("p (h d) -> p h d", h=8)
+            u3 = w[:, 512:1024].rearrange("p (h d) -> p h d", h=8)
+            v3 = w[:, 1024:1536].rearrange("p (h d) -> p h d", h=8)
+            cb = trig[:, a * 64:(a + 1) * 64].unsqueeze(1).to_broadcast([P, 8, 64])
+            s_lo = trig[:, 256 + a * 64:256 + a * 64 + 32].unsqueeze(1).to_broadcast([P, 8, 32])
+            s_hi = trig[:, 256 + a * 64 + 32:256 + a * 64 + 64].unsqueeze(1).to_broadcast([P, 8, 32])
+            eng = nc.gpsimd if USE_G else nc.vector
+            eng.tensor_tensor(out=u3, in0=t3, in1=cb, op=ALU.mult)
+            return t3, v3, s_lo, s_hi
+
+        def epi_c(hc, tt):
+            w = tuv[(hc, tt)]
+            o = otile[(hc, tt)]
+            o3 = o[:].rearrange("p (h d) -> p h d", h=8)
+            u3 = w[:, 512:1024].rearrange("p (h d) -> p h d", h=8)
+            v3 = w[:, 1024:1536].rearrange("p (h d) -> p h d", h=8)
+            t3 = w[:, 0:512].rearrange("p (h d) -> p h d", h=8)
+            a = tt % 4
+            s_lo = trig[:, 256 + a * 64:256 + a * 64 + 32].unsqueeze(1).to_broadcast([P, 8, 32])
+            s_hi = trig[:, 256 + a * 64 + 32:256 + a * 64 + 64].unsqueeze(1).to_broadcast([P, 8, 32])
+            nc.vector.tensor_tensor(out=v3[:, :, 0:32], in0=t3[:, :, 32:64], in1=s_lo, op=ALU.mult)
+            nc.vector.tensor_tensor(out=v3[:, :, 32:64], in0=t3[:, :, 0:32], in1=s_hi, op=ALU.mult)
+            nc.vector.tensor_tensor(out=o3[:, :, 64:128], in0=u3, in1=v3, op=ALU.add)
+            nc.sync.dma_start(out=out_flat[tt * P:(tt + 1) * P, hc * 1024:(hc + 1) * 1024], in_=o[:])
+
+        def rope_tables():
+            pos_i = slot([P, 4], I32, "pos_i")
+            n_i = slot([P, 256], I32, "n_i")
+            scr = slot([P, 2048], F32, "scr")
+            nc.gpsimd.iota(pos_i[:], pattern=[[P, 4]], base=0, channel_multiplier=1)
+            pos_f = scr[:, 0:4]
+            nc.vector.tensor_copy(out=pos_f, in_=pos_i[:])
+            tr = scr[:, 256:512]
+            tr4 = tr.rearrange("p (s a j) -> p s a j", s=2, a=4)
+            for j in range(32):
+                nc.vector.tensor_scalar(
+                    out=tr4[:, 0, :, j], in0=pos_f,
+                    scalar1=10000.0 ** (-j / 32.0) / (2.0 * PI), scalar2=None, op0=ALU.mult,
+                )
+            nc.vector.tensor_scalar(out=tr4[:, 1, :, :], in0=tr4[:, 0, :, :], scalar1=0.25, scalar2=None, op0=ALU.add)
+            nc.vector.tensor_copy(out=n_i[:], in_=tr)
+            nf = scr[:, 512:768]
+            nc.vector.tensor_copy(out=nf, in_=n_i[:])
+            f0 = scr[:, 768:1024]
+            nc.vector.tensor_tensor(out=f0, in0=tr, in1=nf, op=ALU.subtract)
+            m = scr[:, 1024:1280]
+            nc.vector.tensor_single_scalar(out=m, in_=f0, scalar=0.5, op=ALU.is_gt)
+            f1 = scr[:, 1280:1536]
+            nc.vector.tensor_tensor(out=f1, in0=f0, in1=m, op=ALU.subtract)
+            a1 = scr[:, 1536:1792]
+            nc.vector.tensor_scalar(out=a1, in0=f1, scalar1=-1.0, scalar2=0.5, op0=ALU.mult, op1=ALU.add)
+            g1 = scr[:, 1792:2048]
+            nc.vector.tensor_tensor(out=g1, in0=f1, in1=a1, op=ALU.min)
+            a2 = scr[:, 512:768]
+            nc.vector.tensor_scalar(out=a2, in0=f1, scalar1=-1.0, scalar2=-0.5, op0=ALU.mult, op1=ALU.add)
+            g2 = scr[:, 768:1024]
+            nc.vector.tensor_tensor(out=g2, in0=g1, in1=a2, op=ALU.max)
+            g4 = g2.rearrange("p (s a j) -> p s a j", s=2, a=4)
+            cb = trig[:, 0:256].rearrange("p (a f j) -> p a f j", a=4, f=2)
+            sn = trig[:, 256:512].rearrange("p (a f j) -> p a f j", a=4, f=2)
+            two_pi = 2.0 * PI
+            nc.scalar.activation(out=sn[:, :, 0, :], in_=g4[:, 0, :, :], func=ACT.Sin, scale=-two_pi)
+            nc.scalar.activation(out=sn[:, :, 1, :], in_=g4[:, 0, :, :], func=ACT.Sin, scale=two_pi)
+            nc.scalar.activation(out=cb[:, :, 0, :], in_=g4[:, 1, :, :], func=ACT.Sin, scale=two_pi)
+            nc.scalar.activation(out=cb[:, :, 1, :], in_=g4[:, 1, :, :], func=ACT.Sin, scale=two_pi)
+
+        def load_bias2():
+            for which, b in ((0, bq_u), (1, brq)):
+                t = slot([P, 4096], BF16, "bias2")
+                bias2[which] = t
+                nc.sync.dma_start(out=t[:], in_=b.partition_broadcast(P))
+
+        prog = []
+        where = {}
+        for i in range(NRUN):
+            where[runs[i]] = i
+        todo = []
+        for c in range(4):
+            for hf in (0, 1):
+                for grp in range(KH):
+                    need = max(where[("wd", grp, hf)], where[("x", 4 * c + 3, hf)])
+                    todo.append((grp, c, 8 * hf, 8 * hf + 8, need))
+        for grp in range(KH, 16):
+            for c in range(4):
+                todo.append((grp, c, 0, 16, 0))
+        done = [0, 0]
+
+        def take(limit, ready, upto):
+            n = 0
+            while done[0] < len(todo):
+                grp, c, g0, g1, need = todo[done[0]]
+                if upto is not None and (grp, c) > upto:
+                    break
+                if upto is None and (need > ready or n >= limit):
+                    break
+                ga = g0 + done[1]
+                gb = g1 if upto is not None else min(g1, ga + limit - n)
+                prog.append(("M1", grp, c, ga, gb))
+                n += gb - ga
+                if gb == g1:
+                    done[0] += 1
+                    done[1] = 0
+                else:
+                    done[1] = gb - g0
+
+        for i in range(NHEAD):
+            prog.append(("T", i))
+            take(MAXP, i - LAG, None)
+        nxt = NHEAD
+        for grp in range(KH, 16):
+            for hf in (0, 1):
+                prog.append(("T", nxt))
+                nxt += 1
+                take(0, 0, (grp - 1, 2 * hf + 1))
+        for c in range(4):
+            prog.append(("T", nxt))
+            nxt += 1
+            take(0, 0, (15, c))
+            if c == 1:
+                prog.append(("B2",))
+        for hc in range(8):
+            for qd in range(4):
+                if hc < 7:
+                    prog.append(("T", nxt))
+                    nxt += 1
+                for tt in range(4 * qd, 4 * qd + 4):
+                    prog.append(("M2", hc, tt))
+        assert nxt == NRUN
+
+        later = []
+
+        def defer(n, fn):
+            later.append([n + 1, fn])
+
+        def tick():
+            due = []
+            keep = []
+            for e in later:
+                e[0] -= 1
+                if e[0] <= 0:
+                    due.append(e)
+                else:
+                    keep.append(e)
+            later[:] = keep
+            for e in due:
+                e[1]()
+
+        loaded = [0]
+        pend = []
+
+        def load_upto(n):
+            while loaded[0] < min(n, NRUN):
+                load(loaded[0])
+                loaded[0] += 1
+
+        load_upto(LD_HEAD)
+        nc.sync.dma_start(
+            out=bqd_sb[:].rearrange("p (g t) -> p g t", g=4),
+            in_=bq_d.rearrange("(g m t) -> m g t", g=4, t=4),
+        )
+        rope_tables()
+        sort(0, False)
+
+        for item in prog:
+            if item[0] == "T":
+                i = item[1]
+                transp(i)
+                copyout(i)
+                if i + 1 < NRUN:
+                    load_upto(i + 2)
+                    sort(i + 1, runs[i + 1][0] == "w2")
+                load_upto(i + 1 + (LD_HEAD if i < NHEAD - 2 else LD_STEADY))
+                defer(QLAG, lambda i=i: quant(i))
+            elif item[0] == "M1":
+                grp, c, g0, g1 = item[1], item[2], item[3], item[4]
+                mm1(grp, c, g0, g1)
+                if g1 == 16:
+                    evac1(grp, c)
+                    if grp % 4 == 3:
+                        defer(1, lambda gl=grp // 4, c=c: quant_q(gl, c))
+            elif item[0] == "B2":
+                load_bias2()
+            else:
+                hc, tt = item[1], item[2]
+                mm2(hc, tt)
+                if len(pend) > 0:
+                    epi_b(pend[0][0], pend[0][1])
+                epi_a(hc, tt)
+                if len(pend) > 0:
+                    epi_c(pend[0][0], pend[0][1])
+                    pend.pop(0)
+                pend.append((hc, tt))
+            tick()
+        while len(later) > 0:
+            tick()
+        epi_b(pend[0][0], pend[0][1])
+        epi_c(pend[0][0], pend[0][1])

@@ -17,13 +17,15 @@ ACT = mybir.ActivationFunctionType
 P = 128
 PI = 3.141592653589793
 NSLOT = 25
-USE_G = True
+GH = 0
+TT_ORDER = (0, 4, 1, 5, 2, 6, 3, 7, 8, 12, 9, 13, 10, 14, 11, 15)
 LD_HEAD = 3
 LD_STEADY = 2
 QLAG = 1
 KH = 3
 MAXP = 8
 LAG = 2
+SSH = 0
 
 
 def tile_multiheadlatentattention_pa_l_kernel(tc, x, Wq_d, bq_d, Wq_u, bq_u, Wrq, brq, out):
@@ -49,14 +51,15 @@ def tile_multiheadlatentattention_pa_l_kernel(tc, x, Wq_d, bq_d, Wq_u, bq_u, Wrq
         runs = []
         for hf in (0, 1):
             runs.append(("wd", 0, hf))
-            for rt in range(4):
-                runs.append(("x", rt, hf))
+            for kq in (2 * hf, 2 * hf + 1):
+                for rp in (0, 1):
+                    runs.append(("x", rp, kq))
             for grp in range(1, KH):
                 runs.append(("wd", grp, hf))
         for c in (1, 2, 3):
-            for hf in (0, 1):
-                for rt in range(4):
-                    runs.append(("x", 4 * c + rt, hf))
+            for kq in range(4):
+                for rp in (0, 1):
+                    runs.append(("x", 2 * c + rp, kq))
         NHEAD = len(runs)
         for grp in range(KH, 16):
             for hf in (0, 1):
@@ -83,27 +86,30 @@ def tile_multiheadlatentattention_pa_l_kernel(tc, x, Wq_d, bq_d, Wq_u, bq_u, Wrq
             kind, a, b = runs[i]
             r = slot([P, 4096], BF16, "raw")
             raw[i] = r
-            if kind == "x":
-                nc.sync.dma_start(out=r[:], in_=x_flat[a * P:(a + 1) * P, b * 4096:(b + 1) * 4096])
-            elif kind == "wd":
+            if kind == "wd":
                 nc.sync.dma_start(out=r[:], in_=wd_view[a // 4, a % 4][:, b * 4096:(b + 1) * 4096])
             else:
-                w = Wq_u if a % 2 == 0 else Wrq
-                r0 = (a // 2) * 512 + b * 256
+                if kind == "x":
+                    rows = x_flat[a * 256:(a + 1) * 256, b * 2048:(b + 1) * 2048]
+                else:
+                    w = Wq_u if a % 2 == 0 else Wrq
+                    r0 = (a // 2) * 512 + b * 256
+                    rows = w[r0:r0 + 256, :]
                 nc.sync.dma_start(
                     out=r[:].rearrange("p (r k) -> p r k", r=2),
-                    in_=w[r0:r0 + 256, :].rearrange("(r p) k -> p r k", p=P),
+                    in_=rows.rearrange("(r p) k -> p r k", p=P),
                 )
 
-        def sort(i, on_scalar):
+        def sort(i, n_scalar):
             s = slot([P, 2048], F32, "srt")
             srt[i] = s
             dst = s[:].rearrange("p (b u q) -> p b u q", b=8, u=2)
             src = raw[i][:].bitcast(F32).rearrange("p (b q u) -> p b u q", b=8, u=2)
-            if on_scalar:
-                nc.scalar.copy(out=dst, in_=src)
-            else:
-                nc.vector.tensor_copy(out=dst, in_=src)
+            nv = 8 - n_scalar
+            if nv > 0:
+                nc.vector.tensor_copy(out=dst[:, 0:nv], in_=src[:, 0:nv])
+            if n_scalar > 0:
+                nc.scalar.copy(out=dst[:, nv:8], in_=src[:, nv:8])
 
         def transp(i):
             banks = []
@@ -120,10 +126,13 @@ def tile_multiheadlatentattention_pa_l_kernel(tc, x, Wq_d, bq_d, Wq_u, bq_u, Wrq
             grpd[i] = g
             gw = g[:].bitcast(F32)
             for k in range(4):
-                nc.scalar.copy(
-                    out=gw[:, k * 512:(k + 1) * 512].rearrange("p (b r u) -> p b r u", b=2, u=2),
-                    in_=tps[i][k][:].rearrange("p (b u) r -> p b r u", u=2),
-                )
+                if runs[i][0] == "wd":
+                    dst = gw[:, k * 512:(k + 1) * 512].rearrange("p (b r u) -> p b r u", b=2, u=2)
+                else:
+                    g0 = 2 * (k % 2)
+                    dst = gw.rearrange("p (g r w) -> p g r w", g=4, r=2)[:, g0:g0 + 2, k // 2, :]
+                    dst = dst.rearrange("p b (r u) -> p b r u", u=2)
+                nc.scalar.copy(out=dst, in_=tps[i][k][:].rearrange("p (b u) r -> p b r u", u=2))
 
         def quant(i):
             kind, a, b = runs[i]
@@ -139,32 +148,30 @@ def tile_multiheadlatentattention_pa_l_kernel(tc, x, Wq_d, bq_d, Wq_u, bq_u, Wrq
                         scales=wp[a][4 * j:P, :],
                         in_=g[:, j2 * 2048:(j2 + 1) * 2048],
                     )
-            elif kind == "x":
-                c, rt = a // 4, a % 4
-                if rt == 0 and b == 0:
-                    xp[c] = sb.tile([P, 2048], U8, name="xp", tag="xp", bufs=4, align_bytes=64)
-                for blk in range(8):
-                    gp = b * 8 + blk
-                    j = gp // 4
-                    if rt == 0 and gp % 4 == 0:
-                        xc[(c, j)] = slot([P, 2048], U32, "xc")
-                    c0 = (gp % 4) * 512 + rt * P
-                    nc.vector.quantize_mx(
-                        out=xc[(c, j)][:, c0:c0 + P].bitcast(FP8X4),
-                        scales=xp[c][4 * j:P, c0:c0 + P],
-                        in_=g[:, blk * 512:(blk + 1) * 512],
-                    )
             else:
-                if b == 0:
-                    uc[a] = slot([P, 2048], U32, "uc")
-                    up[a] = sb.tile([P, 512], U8, name="up", tag="wp", bufs=4, align_bytes=64)
-                for blk in range(8):
-                    r, gl = blk // 4, blk % 4
-                    c0 = (b * 2 + r) * P
+                if kind == "x":
+                    c, rp, j = a // 2, a % 2, b
+                    if rp == 0 and j == 0:
+                        xp[c] = sb.tile([P, 2048], U8, name="xp", tag="xp", bufs=4, align_bytes=64)
+                    if rp == 0:
+                        xc[(c, j)] = slot([P, 2048], U32, "xc")
+                    codes, plane = xc[(c, j)], xp[c]
+                else:
+                    rp = b
+                    if rp == 0:
+                        uc[a] = slot([P, 2048], U32, "uc")
+                        up[a] = sb.tile([P, 512], U8, name="up", tag="wp", bufs=4, align_bytes=64)
+                    codes, plane = uc[a], up[a]
+                for gl in range(4):
+                    c0 = gl * 512 + rp * 256
+                    if kind == "x":
+                        sc = plane[4 * j:P, c0:c0 + 256]
+                    else:
+                        sc = plane[4 * gl:P, rp * 256:rp * 256 + 256]
                     nc.vector.quantize_mx(
-                        out=uc[a][:, gl * 512 + c0:gl * 512 + c0 + P].bitcast(FP8X4),
-                        scales=up[a][4 * gl:P, c0:c0 + P],
-                        in_=g[:, blk * 512:(blk + 1) * 512],
+                        out=codes[:, c0:c0 + 256].bitcast(FP8X4),
+                        scales=sc,
+                        in_=g[:, gl * 1024:(gl + 1) * 1024],
                     )
 
         acc1 = {}
@@ -210,6 +217,7 @@ def tile_multiheadlatentattention_pa_l_kernel(tc, x, Wq_d, bq_d, Wq_u, bq_u, Wrq
         bias2 = {}
         tuv = {}
         otile = {}
+        utile = {}
 
         def mm2(hc, tt):
             for which in (1, 0):
@@ -227,52 +235,63 @@ def tile_multiheadlatentattention_pa_l_kernel(tc, x, Wq_d, bq_d, Wq_u, bq_u, Wrq
                         stop=(gl == 3),
                     )
 
-        def epi_a(hc, tt):
-            o = slot([P, 1024], F32, "o")
-            otile[(hc, tt)] = o
-            o3 = o[:].rearrange("p (h d) -> p h d", h=8)
-            w = slot([P, 1536], F32, "tuv")
-            tuv[(hc, tt)] = w
+        def heads(ap, n):
+            return ap.rearrange("p (h d) -> p h d", h=n)
+
+        def table(col, width, n):
+            return trig[:, col:col + width].unsqueeze(1).to_broadcast([P, n, width])
+
+        def epi_bias(hc, tt, half):
+            key = (hc, tt - 4 * half)
+            if half == 0:
+                otile[key] = slot([P, 2048], F32, "o")
+                tuv[key] = slot([P, 2048], F32, "tv")
             nc.vector.tensor_tensor(
-                out=w[:, 0:512],
+                out=tuv[key][:, half * 512:(half + 1) * 512],
                 in0=acc2[(hc, tt, 1)][:],
                 in1=bias2[1][:, hc * 512:(hc + 1) * 512],
                 op=ALU.add,
             )
             nc.vector.tensor_tensor(
-                out=o3[:, :, 0:64],
-                in0=acc2[(hc, tt, 0)][:].rearrange("p (h d) -> p h d", h=8),
-                in1=bias2[0][:, hc * 512:(hc + 1) * 512].rearrange("p (h d) -> p h d", h=8),
+                out=heads(otile[key][:, half * 1024:(half + 1) * 1024], 8)[:, :, 0:64],
+                in0=heads(acc2[(hc, tt, 0)][:], 8),
+                in1=heads(bias2[0][:, hc * 512:(hc + 1) * 512], 8),
                 op=ALU.add,
             )
 
-        def epi_b(hc, tt):
-            a = tt % 4
-            w = tuv[(hc, tt)]
-            t3 = w[:, 0:512].rearrange("p (h d) -> p h d", h=8)
-            u3 = w[:, 512:1024].rearrange("p (h d) -> p h d", h=8)
-            v3 = w[:, 1024:1536].rearrange("p (h d) -> p h d", h=8)
-            cb = trig[:, a * 64:(a + 1) * 64].unsqueeze(1).to_broadcast([P, 8, 64])
-            s_lo = trig[:, 256 + a * 64:256 + a * 64 + 32].unsqueeze(1).to_broadcast([P, 8, 32])
-            s_hi = trig[:, 256 + a * 64 + 32:256 + a * 64 + 64].unsqueeze(1).to_broadcast([P, 8, 32])
-            eng = nc.gpsimd if USE_G else nc.vector
-            eng.tensor_tensor(out=u3, in0=t3, in1=cb, op=ALU.mult)
-            return t3, v3, s_lo, s_hi
+        def epi_sin(key):
+            a = key[1] % 4
+            t3 = heads(tuv[key][:, 0:1024], 16)
+            v3 = heads(tuv[key][:, 1024:2048], 16)
+            nc.vector.tensor_tensor(out=v3[:, :, 0:32], in0=t3[:, :, 32:64], in1=table(256 + a * 64, 32, 16), op=ALU.mult)
+            nc.vector.tensor_tensor(out=v3[:, :, 32:64], in0=t3[:, :, 0:32], in1=table(256 + a * 64 + 32, 32, 16), op=ALU.mult)
 
-        def epi_c(hc, tt):
-            w = tuv[(hc, tt)]
-            o = otile[(hc, tt)]
-            o3 = o[:].rearrange("p (h d) -> p h d", h=8)
-            u3 = w[:, 512:1024].rearrange("p (h d) -> p h d", h=8)
-            v3 = w[:, 1024:1536].rearrange("p (h d) -> p h d", h=8)
-            t3 = w[:, 0:512].rearrange("p (h d) -> p h d", h=8)
-            a = tt % 4
-            s_lo = trig[:, 256 + a * 64:256 + a * 64 + 32].unsqueeze(1).to_broadcast([P, 8, 32])
-            s_hi = trig[:, 256 + a * 64 + 32:256 + a * 64 + 64].unsqueeze(1).to_broadcast([P, 8, 32])
-            nc.vector.tensor_tensor(out=v3[:, :, 0:32], in0=t3[:, :, 32:64], in1=s_lo, op=ALU.mult)
-            nc.vector.tensor_tensor(out=v3[:, :, 32:64], in0=t3[:, :, 0:32], in1=s_hi, op=ALU.mult)
-            nc.vector.tensor_tensor(out=o3[:, :, 64:128], in0=u3, in1=v3, op=ALU.add)
-            nc.sync.dma_start(out=out_flat[tt * P:(tt + 1) * P, hc * 1024:(hc + 1) * 1024], in_=o[:])
+        def epi_cos(key):
+            a = key[1] % 4
+            u = sb.tile([P, 1024], F32, name="u", tag="u", bufs=1)
+            utile[key] = u
+            t3 = heads(tuv[key][:, 0:1024], 16)
+            u3 = heads(u[:], 16)
+            if GH < 16:
+                nc.vector.tensor_tensor(out=u3[:, GH:16, :], in0=t3[:, GH:16, :], in1=table(a * 64, 64, 16 - GH), op=ALU.mult)
+            if GH > 0:
+                nc.gpsimd.tensor_tensor(out=u3[:, 0:GH, :], in0=t3[:, 0:GH, :], in1=table(a * 64, 64, GH), op=ALU.mult)
+
+        def epi_sum(key):
+            hc, tt = key
+            o = otile[key]
+            nc.vector.tensor_tensor(
+                out=heads(o[:], 16)[:, :, 64:128],
+                in0=heads(utile[key][:], 16),
+                in1=heads(tuv[key][:, 1024:2048], 16),
+                op=ALU.add,
+            )
+            for half in (0, 1):
+                t0 = (tt + 4 * half) * P
+                nc.sync.dma_start(
+                    out=out_flat[t0:t0 + P, hc * 1024:(hc + 1) * 1024],
+                    in_=o[:, half * 1024:(half + 1) * 1024],
+                )
 
         def rope_tables():
             pos_i = slot([P, 4], I32, "pos_i")
@@ -329,8 +348,9 @@ def tile_multiheadlatentattention_pa_l_kernel(tc, x, Wq_d, bq_d, Wq_u, bq_u, Wrq
         for c in range(4):
             for hf in (0, 1):
                 for grp in range(KH):
-                    need = max(where[("wd", grp, hf)], where[("x", 4 * c + 3, hf)])
-                    todo.append((grp, c, 8 * hf, 8 * hf + 8, need))
+                    for j in (2 * hf, 2 * hf + 1):
+                        need = max(where[("wd", grp, hf)], where[("x", 2 * c + 1, j)])
+                        todo.append((grp, c, 4 * j, 4 * j + 4, need))
         for grp in range(KH, 16):
             for c in range(4):
                 todo.append((grp, c, 0, 16, 0))
@@ -374,7 +394,7 @@ def tile_multiheadlatentattention_pa_l_kernel(tc, x, Wq_d, bq_d, Wq_u, bq_u, Wrq
                 if hc < 7:
                     prog.append(("T", nxt))
                     nxt += 1
-                for tt in range(4 * qd, 4 * qd + 4):
+                for tt in TT_ORDER[4 * qd:4 * qd + 4]:
                     prog.append(("M2", hc, tt))
         assert nxt == NRUN
 
@@ -410,7 +430,7 @@ def tile_multiheadlatentattention_pa_l_kernel(tc, x, Wq_d, bq_d, Wq_u, bq_u, Wrq
             in_=bq_d.rearrange("(g m t) -> m g t", g=4, t=4),
         )
         rope_tables()
-        sort(0, False)
+        sort(0, 0)
 
         for item in prog:
             if item[0] == "T":
@@ -419,7 +439,7 @@ def tile_multiheadlatentattention_pa_l_kernel(tc, x, Wq_d, bq_d, Wq_u, bq_u, Wrq
                 copyout(i)
                 if i + 1 < NRUN:
                     load_upto(i + 2)
-                    sort(i + 1, runs[i + 1][0] == "w2")
+                    sort(i + 1, 8 if runs[i + 1][0] == "w2" else (SSH if i + 1 < NHEAD else 0))
                 load_upto(i + 1 + (LD_HEAD if i < NHEAD - 2 else LD_STEADY))
                 defer(QLAG, lambda i=i: quant(i))
             elif item[0] == "M1":
@@ -433,16 +453,17 @@ def tile_multiheadlatentattention_pa_l_kernel(tc, x, Wq_d, bq_d, Wq_u, bq_u, Wrq
                 load_bias2()
             else:
                 hc, tt = item[1], item[2]
+                half = (tt // 4) % 2
                 mm2(hc, tt)
-                if len(pend) > 0:
-                    epi_b(pend[0][0], pend[0][1])
-                epi_a(hc, tt)
-                if len(pend) > 0:
-                    epi_c(pend[0][0], pend[0][1])
-                    pend.pop(0)
-                pend.append((hc, tt))
+                epi_bias(hc, tt, half)
+                if half == 1:
+                    key = (hc, tt - 4)
+                    epi_sin(key)
+                    if len(pend) > 0:
+                        epi_sum(pend.pop(0))
+                    epi_cos(key)
+                    pend.append(key)
             tick()
         while len(later) > 0:
             tick()
-        epi_b(pend[0][0], pend[0][1])
-        epi_c(pend[0][0], pend[0][1])
+        epi_sum(pend.pop(0))

@@ -17,7 +17,7 @@ ACT = mybir.ActivationFunctionType
 P = 128
 PI = 3.141592653589793
 NSLOT = 25
-GH = 0
+GH = 8
 TT_ORDER = (0, 4, 1, 5, 2, 6, 3, 7, 8, 12, 9, 13, 10, 14, 11, 15)
 LD_HEAD = 3
 LD_STEADY = 2

@@ -17,8 +17,8 @@ ACT = mybir.ActivationFunctionType
 P = 128
 PI = 3.141592653589793
 NSLOT = 25
-GH = 8
-TT_ORDER = (0, 4, 1, 5, 2, 6, 3, 7, 8, 12, 9, 13, 10, 14, 11, 15)
+GH = 10
+TT_FIRST = (0, 1, 2, 3, 8, 9, 10, 11)
 LD_HEAD = 3
 LD_STEADY = 2
 QLAG = 1
@@ -26,6 +26,7 @@ KH = 3
 MAXP = 8
 LAG = 2
 SSH = 0
+ROPE_AT = (5, 0)
 
 
 def tile_multiheadlatentattention_pa_l_kernel(tc, x, Wq_d, bq_d, Wq_u, bq_u, Wrq, brq, out):
@@ -81,6 +82,7 @@ def tile_multiheadlatentattention_pa_l_kernel(tc, x, Wq_d, bq_d, Wq_u, bq_u, Wrq
         xp = {}
         qc = {}
         qg = {}
+        qi = {}
 
         def load(i):
             kind, a, b = runs[i]
@@ -197,11 +199,18 @@ def tile_multiheadlatentattention_pa_l_kernel(tc, x, Wq_d, bq_d, Wq_u, bq_u, Wrq
             if t == 0:
                 qg[c] = sb.tile([P, 2048], BF16, name="qg", tag="qg", bufs=4, align_bytes=64)
             nc.scalar.activation(
-                out=qg[c][:].rearrange("p (n t) -> p n t", t=4)[:, :, t],
+                out=qg[c][:, t * 512:(t + 1) * 512],
                 in_=acc1[(grp, c)][:],
                 func=ACT.Identity,
                 bias=bqd_sb[:, grp:grp + 1],
                 scale=1.0,
+            )
+
+        def weave_q(c):
+            qi[c] = sb.tile([P, 2048], BF16, name="qi", tag="u", bufs=1, align_bytes=64)
+            nc.vector.tensor_copy(
+                out=qi[c][:].rearrange("p (n t) -> p n t", t=4),
+                in_=qg[c][:].rearrange("p (t n) -> p n t", t=4),
             )
 
         def quant_q(gl, c):
@@ -210,7 +219,7 @@ def tile_multiheadlatentattention_pa_l_kernel(tc, x, Wq_d, bq_d, Wq_u, bq_u, Wrq
             nc.vector.quantize_mx(
                 out=qc[gl][:, c * 512:(c + 1) * 512].bitcast(FP8X4),
                 scales=qp[4 * gl:P, c * 512:(c + 1) * 512],
-                in_=qg[c][:],
+                in_=qi[c][:],
             )
 
         acc2 = {}
@@ -219,8 +228,8 @@ def tile_multiheadlatentattention_pa_l_kernel(tc, x, Wq_d, bq_d, Wq_u, bq_u, Wrq
         otile = {}
         utile = {}
 
-        def mm2(hc, tt):
-            for which in (1, 0):
+        def mm2(hc, tt, which):
+            if True:
                 a = ps.tile([P, 512], F32, name="acc", tag="acc", bufs=4)
                 acc2[(hc, tt, which)] = a
                 u = hc * 2 + which
@@ -241,23 +250,26 @@ def tile_multiheadlatentattention_pa_l_kernel(tc, x, Wq_d, bq_d, Wq_u, bq_u, Wrq
         def table(col, width, n):
             return trig[:, col:col + width].unsqueeze(1).to_broadcast([P, n, width])
 
-        def epi_bias(hc, tt, half):
+        def epi_bias(hc, tt, half, which):
             key = (hc, tt - 4 * half)
-            if half == 0:
-                otile[key] = slot([P, 2048], F32, "o")
-                tuv[key] = slot([P, 2048], F32, "tv")
-            nc.vector.tensor_tensor(
-                out=tuv[key][:, half * 512:(half + 1) * 512],
-                in0=acc2[(hc, tt, 1)][:],
-                in1=bias2[1][:, hc * 512:(hc + 1) * 512],
-                op=ALU.add,
-            )
-            nc.vector.tensor_tensor(
-                out=heads(otile[key][:, half * 1024:(half + 1) * 1024], 8)[:, :, 0:64],
-                in0=heads(acc2[(hc, tt, 0)][:], 8),
-                in1=heads(bias2[0][:, hc * 512:(hc + 1) * 512], 8),
-                op=ALU.add,
-            )
+            if which == 1:
+                if half == 0:
+                    tuv[key] = slot([P, 2048], F32, "tv")
+                nc.vector.tensor_tensor(
+                    out=tuv[key][:, half * 512:(half + 1) * 512],
+                    in0=acc2[(hc, tt, 1)][:],
+                    in1=bias2[1][:, hc * 512:(hc + 1) * 512],
+                    op=ALU.add,
+                )
+            else:
+                if half == 0:
+                    otile[key] = slot([P, 2048], F32, "o")
+                nc.vector.tensor_tensor(
+                    out=heads(otile[key][:, half * 1024:(half + 1) * 1024], 8)[:, :, 0:64],
+                    in0=heads(acc2[(hc, tt, 0)][:], 8),
+                    in1=heads(bias2[0][:, hc * 512:(hc + 1) * 512], 8),
+                    op=ALU.add,
+                )
 
         def epi_sin(key):
             a = key[1] % 4
@@ -268,14 +280,14 @@ def tile_multiheadlatentattention_pa_l_kernel(tc, x, Wq_d, bq_d, Wq_u, bq_u, Wrq
 
         def epi_cos(key):
             a = key[1] % 4
-            u = sb.tile([P, 1024], F32, name="u", tag="u", bufs=1)
+            gh = GH
+            u = sb.tile([P, 1024], F32, name="u", tag="u", bufs=1, align_bytes=64)
             utile[key] = u
             t3 = heads(tuv[key][:, 0:1024], 16)
             u3 = heads(u[:], 16)
-            if GH < 16:
-                nc.vector.tensor_tensor(out=u3[:, GH:16, :], in0=t3[:, GH:16, :], in1=table(a * 64, 64, 16 - GH), op=ALU.mult)
-            if GH > 0:
-                nc.gpsimd.tensor_tensor(out=u3[:, 0:GH, :], in0=t3[:, 0:GH, :], in1=table(a * 64, 64, GH), op=ALU.mult)
+            nc.vector.tensor_tensor(out=u3[:, gh:16, :], in0=t3[:, gh:16, :], in1=table(a * 64, 64, 16 - gh), op=ALU.mult)
+            if gh > 0:
+                nc.gpsimd.tensor_tensor(out=u3[:, 0:gh, :], in0=t3[:, 0:gh, :], in1=table(a * 64, 64, gh), op=ALU.mult)
 
         def epi_sum(key):
             hc, tt = key
@@ -294,13 +306,17 @@ def tile_multiheadlatentattention_pa_l_kernel(tc, x, Wq_d, bq_d, Wq_u, bq_u, Wrq
                 )
 
         def rope_tables():
-            pos_i = slot([P, 4], I32, "pos_i")
-            n_i = slot([P, 256], I32, "n_i")
             scr = slot([P, 2048], F32, "scr")
-            nc.gpsimd.iota(pos_i[:], pattern=[[P, 4]], base=0, channel_multiplier=1)
+
+            def reg(n):
+                return scr[:, 256 * n:256 * (n + 1)]
+
+            pos_i = sb.tile([P, 4], I32, name="pos_i")
+            n_i = sb.tile([P, 256], I32, name="n_i")
             pos_f = scr[:, 0:4]
+            nc.gpsimd.iota(pos_i[:], pattern=[[P, 4]], base=0, channel_multiplier=1)
             nc.vector.tensor_copy(out=pos_f, in_=pos_i[:])
-            tr = scr[:, 256:512]
+            tr = reg(1)
             tr4 = tr.rearrange("p (s a j) -> p s a j", s=2, a=4)
             for j in range(32):
                 nc.vector.tensor_scalar(
@@ -309,21 +325,21 @@ def tile_multiheadlatentattention_pa_l_kernel(tc, x, Wq_d, bq_d, Wq_u, bq_u, Wrq
                 )
             nc.vector.tensor_scalar(out=tr4[:, 1, :, :], in0=tr4[:, 0, :, :], scalar1=0.25, scalar2=None, op0=ALU.add)
             nc.vector.tensor_copy(out=n_i[:], in_=tr)
-            nf = scr[:, 512:768]
+            nf = reg(3)
             nc.vector.tensor_copy(out=nf, in_=n_i[:])
-            f0 = scr[:, 768:1024]
+            f0 = reg(4)
             nc.vector.tensor_tensor(out=f0, in0=tr, in1=nf, op=ALU.subtract)
-            m = scr[:, 1024:1280]
+            m = reg(5)
             nc.vector.tensor_single_scalar(out=m, in_=f0, scalar=0.5, op=ALU.is_gt)
-            f1 = scr[:, 1280:1536]
+            f1 = reg(6)
             nc.vector.tensor_tensor(out=f1, in0=f0, in1=m, op=ALU.subtract)
-            a1 = scr[:, 1536:1792]
+            a1 = reg(7)
             nc.vector.tensor_scalar(out=a1, in0=f1, scalar1=-1.0, scalar2=0.5, op0=ALU.mult, op1=ALU.add)
-            g1 = scr[:, 1792:2048]
+            g1 = reg(2)
             nc.vector.tensor_tensor(out=g1, in0=f1, in1=a1, op=ALU.min)
-            a2 = scr[:, 512:768]
+            a2 = reg(3)
             nc.vector.tensor_scalar(out=a2, in0=f1, scalar1=-1.0, scalar2=-0.5, op0=ALU.mult, op1=ALU.add)
-            g2 = scr[:, 768:1024]
+            g2 = reg(4)
             nc.vector.tensor_tensor(out=g2, in0=g1, in1=a2, op=ALU.max)
             g4 = g2.rearrange("p (s a j) -> p s a j", s=2, a=4)
             cb = trig[:, 0:256].rearrange("p (a f j) -> p a f j", a=4, f=2)
@@ -383,6 +399,8 @@ def tile_multiheadlatentattention_pa_l_kernel(tc, x, Wq_d, bq_d, Wq_u, bq_u, Wrq
                 prog.append(("T", nxt))
                 nxt += 1
                 take(0, 0, (grp - 1, 2 * hf + 1))
+                if (grp, hf) == ROPE_AT:
+                    prog.append(("ROPE",))
         for c in range(4):
             prog.append(("T", nxt))
             nxt += 1
@@ -394,7 +412,7 @@ def tile_multiheadlatentattention_pa_l_kernel(tc, x, Wq_d, bq_d, Wq_u, bq_u, Wrq
                 if hc < 7:
                     prog.append(("T", nxt))
                     nxt += 1
-                for tt in TT_ORDER[4 * qd:4 * qd + 4]:
+                for tt in TT_FIRST[2 * qd:2 * qd + 2]:
                     prog.append(("M2", hc, tt))
         assert nxt == NRUN
 
@@ -418,6 +436,7 @@ def tile_multiheadlatentattention_pa_l_kernel(tc, x, Wq_d, bq_d, Wq_u, bq_u, Wrq
 
         loaded = [0]
         pend = []
+        wq = []
 
         def load_upto(n):
             while loaded[0] < min(n, NRUN):
@@ -429,7 +448,6 @@ def tile_multiheadlatentattention_pa_l_kernel(tc, x, Wq_d, bq_d, Wq_u, bq_u, Wrq
             out=bqd_sb[:].rearrange("p (g t) -> p g t", g=4),
             in_=bq_d.rearrange("(g m t) -> m g t", g=4, t=4),
         )
-        rope_tables()
         sort(0, 0)
 
         for item in prog:
@@ -441,28 +459,39 @@ def tile_multiheadlatentattention_pa_l_kernel(tc, x, Wq_d, bq_d, Wq_u, bq_u, Wrq
                     load_upto(i + 2)
                     sort(i + 1, 8 if runs[i + 1][0] == "w2" else (SSH if i + 1 < NHEAD else 0))
                 load_upto(i + 1 + (LD_HEAD if i < NHEAD - 2 else LD_STEADY))
-                defer(QLAG, lambda i=i: quant(i))
+                if i >= NRUN - 28:
+                    wq.append(i)
+                else:
+                    defer(QLAG, lambda i=i: quant(i))
             elif item[0] == "M1":
                 grp, c, g0, g1 = item[1], item[2], item[3], item[4]
                 mm1(grp, c, g0, g1)
                 if g1 == 16:
                     evac1(grp, c)
                     if grp % 4 == 3:
-                        defer(1, lambda gl=grp // 4, c=c: quant_q(gl, c))
+                        defer(1, lambda c=c: weave_q(c))
+                        defer(2, lambda gl=grp // 4, c=c: quant_q(gl, c))
+                    if (grp, c) == (15, 3):
+                        while len(later) > 0:
+                            tick()
             elif item[0] == "B2":
                 load_bias2()
+            elif item[0] == "ROPE":
+                rope_tables()
             else:
                 hc, tt = item[1], item[2]
-                half = (tt // 4) % 2
-                mm2(hc, tt)
-                epi_bias(hc, tt, half)
-                if half == 1:
-                    key = (hc, tt - 4)
-                    epi_sin(key)
-                    if len(pend) > 0:
-                        epi_sum(pend.pop(0))
-                    epi_cos(key)
-                    pend.append(key)
+                key = (hc, tt)
+                for which in (1, 0):
+                    for half in (0, 1):
+                        mm2(hc, tt + 4 * half, which)
+                        epi_bias(hc, tt + 4 * half, half, which)
+                epi_sin(key)
+                while len(wq) > 0:
+                    quant(wq.pop(0))
+                if len(pend) > 0:
+                    epi_sum(pend.pop(0))
+                epi_cos(key)
+                pend.append(key)
             tick()
         while len(later) > 0:
             tick()

@@ -16,24 +16,23 @@ ACT = mybir.ActivationFunctionType
 
 P = 128
 PI = 3.141592653589793
-NSLOT = 25
-GH = 10
-TT_FIRST = (0, 1, 2, 3, 8, 9, 10, 11)
-LD_HEAD = 3
-LD_STEADY = 2
-QLAG = 1
-KH = 3
-MAXP = 8
-LAG = 2
-SSH = 0
-ROPE_AT = (5, 0)
+
+SLOTS = 25
+HEAD_GROUPS = 3
+HEAD_PASSES = 8
+READY_LAG = 2
+LOAD_AHEAD_HEAD = 3
+LOAD_AHEAD = 2
+ROPE_AFTER = (5, 0)
+PAIR_FIRST = (0, 1, 2, 3, 8, 9, 10, 11)
+GPSIMD_HEADS = 12
 
 
 def tile_multiheadlatentattention_pa_l_kernel(tc, x, Wq_d, bq_d, Wq_u, bq_u, Wrq, brq, out):
     nc = tc.nc
     x_flat = x.flatten_outer_dims()
     out_flat = out.rearrange("b s h d -> (b s) (h d)")
-    wd_view = Wq_d.rearrange("(g m t) k -> g t m k", g=4, t=4)
+    wd_groups = Wq_d.rearrange("(g m t) k -> g t m k", g=4, t=4)
 
     with ExitStack() as ctx:
         ctx.enter_context(tc.manual_schedule())
@@ -41,7 +40,7 @@ def tile_multiheadlatentattention_pa_l_kernel(tc, x, Wq_d, bq_d, Wq_u, bq_u, Wrq
         ps = ctx.enter_context(tc.psum_pool(name="ps", bufs=4))
 
         def slot(shape, dtype, name):
-            return sb.tile(shape, dtype, name=name, tag="slot", bufs=NSLOT, align_bytes=64)
+            return sb.tile(shape, dtype, name=name, tag="slot", bufs=SLOTS, align_bytes=64)
 
         ident = sb.tile([P, P], F32, name="ident")
         make_identity(nc, ident[:])
@@ -55,41 +54,38 @@ def tile_multiheadlatentattention_pa_l_kernel(tc, x, Wq_d, bq_d, Wq_u, bq_u, Wrq
             for kq in (2 * hf, 2 * hf + 1):
                 for rp in (0, 1):
                     runs.append(("x", rp, kq))
-            for grp in range(1, KH):
+            for grp in range(1, HEAD_GROUPS):
                 runs.append(("wd", grp, hf))
         for c in (1, 2, 3):
             for kq in range(4):
                 for rp in (0, 1):
                     runs.append(("x", 2 * c + rp, kq))
-        NHEAD = len(runs)
-        for grp in range(KH, 16):
+        n_head = len(runs)
+        for grp in range(HEAD_GROUPS, 16):
             for hf in (0, 1):
                 runs.append(("wd", grp, hf))
         for unit in range(16):
             for rp in (0, 1):
                 runs.append(("w2", unit, rp))
-        NRUN = len(runs)
+        n_runs = len(runs)
+        index_of = {}
+        for i in range(n_runs):
+            index_of[runs[i]] = i
 
         raw = {}
         srt = {}
         tps = {}
         grpd = {}
-        wc = {}
-        wp = {}
-        uc = {}
-        up = {}
-        xc = {}
-        xp = {}
-        qc = {}
-        qg = {}
-        qi = {}
+        wc, wp = {}, {}
+        xc, xp = {}, {}
+        uc, up = {}, {}
 
-        def load(i):
+        def load_run(i):
             kind, a, b = runs[i]
             r = slot([P, 4096], BF16, "raw")
             raw[i] = r
             if kind == "wd":
-                nc.sync.dma_start(out=r[:], in_=wd_view[a // 4, a % 4][:, b * 4096:(b + 1) * 4096])
+                nc.sync.dma_start(out=r[:], in_=wd_groups[a // 4, a % 4][:, b * 4096:(b + 1) * 4096])
             else:
                 if kind == "x":
                     rows = x_flat[a * 256:(a + 1) * 256, b * 2048:(b + 1) * 2048]
@@ -102,18 +98,17 @@ def tile_multiheadlatentattention_pa_l_kernel(tc, x, Wq_d, bq_d, Wq_u, bq_u, Wrq
                     in_=rows.rearrange("(r p) k -> p r k", p=P),
                 )
 
-        def sort(i, n_scalar):
+        def sort_run(i):
             s = slot([P, 2048], F32, "srt")
             srt[i] = s
             dst = s[:].rearrange("p (b u q) -> p b u q", b=8, u=2)
             src = raw[i][:].bitcast(F32).rearrange("p (b q u) -> p b u q", b=8, u=2)
-            nv = 8 - n_scalar
-            if nv > 0:
-                nc.vector.tensor_copy(out=dst[:, 0:nv], in_=src[:, 0:nv])
-            if n_scalar > 0:
-                nc.scalar.copy(out=dst[:, nv:8], in_=src[:, nv:8])
+            if runs[i][0] == "w2":
+                nc.scalar.copy(out=dst[:, 0:8], in_=src[:, 0:8])
+            else:
+                nc.vector.tensor_copy(out=dst[:, 0:8], in_=src[:, 0:8])
 
-        def transp(i):
+        def transpose_run(i):
             banks = []
             for k in range(4):
                 t = ps.tile([P, 4, P], F32, name="tp", tag="tp", bufs=4)
@@ -123,7 +118,7 @@ def tile_multiheadlatentattention_pa_l_kernel(tc, x, Wq_d, bq_d, Wq_u, bq_u, Wrq
                     nc.tensor.transpose(out=t[:, s, :], in_=srt[i][:, c0:c0 + P], identity=ident[:])
             tps[i] = banks
 
-        def copyout(i):
+        def copy_out_run(i):
             g = slot([P, 4096], BF16, "grpd")
             grpd[i] = g
             gw = g[:].bitcast(F32)
@@ -136,7 +131,7 @@ def tile_multiheadlatentattention_pa_l_kernel(tc, x, Wq_d, bq_d, Wq_u, bq_u, Wrq
                     dst = dst.rearrange("p b (r u) -> p b r u", u=2)
                 nc.scalar.copy(out=dst, in_=tps[i][k][:].rearrange("p (b u) r -> p b r u", u=2))
 
-        def quant(i):
+        def quantize_run(i):
             kind, a, b = runs[i]
             g = grpd[i]
             if kind == "wd":
@@ -177,8 +172,11 @@ def tile_multiheadlatentattention_pa_l_kernel(tc, x, Wq_d, bq_d, Wq_u, bq_u, Wrq
                     )
 
         acc1 = {}
+        qg = {}
+        qi = {}
+        qc = {}
 
-        def mm1(grp, c, g0, g1):
+        def stage1_passes(grp, c, g0, g1):
             if g0 == 0:
                 acc1[(grp, c)] = ps.tile([P, 512], F32, name="acc", tag="acc", bufs=4)
             a = acc1[(grp, c)]
@@ -194,8 +192,8 @@ def tile_multiheadlatentattention_pa_l_kernel(tc, x, Wq_d, bq_d, Wq_u, bq_u, Wrq
                     stop=(gp == 15),
                 )
 
-        def evac1(grp, c):
-            gl, t = grp // 4, grp % 4
+        def stage1_bias(grp, c):
+            t = grp % 4
             if t == 0:
                 qg[c] = sb.tile([P, 2048], BF16, name="qg", tag="qg", bufs=4, align_bytes=64)
             nc.scalar.activation(
@@ -206,14 +204,14 @@ def tile_multiheadlatentattention_pa_l_kernel(tc, x, Wq_d, bq_d, Wq_u, bq_u, Wrq
                 scale=1.0,
             )
 
-        def weave_q(c):
+        def interleave_q(c):
             qi[c] = sb.tile([P, 2048], BF16, name="qi", tag="u", bufs=1, align_bytes=64)
             nc.vector.tensor_copy(
                 out=qi[c][:].rearrange("p (n t) -> p n t", t=4),
                 in_=qg[c][:].rearrange("p (t n) -> p n t", t=4),
             )
 
-        def quant_q(gl, c):
+        def quantize_q(gl, c):
             if c == 0:
                 qc[gl] = slot([P, 2048], U32, "qc")
             nc.vector.quantize_mx(
@@ -224,25 +222,24 @@ def tile_multiheadlatentattention_pa_l_kernel(tc, x, Wq_d, bq_d, Wq_u, bq_u, Wrq
 
         acc2 = {}
         bias2 = {}
-        tuv = {}
-        otile = {}
-        utile = {}
+        tv = {}
+        cosp = {}
+        o = {}
 
-        def mm2(hc, tt, which):
-            if True:
-                a = ps.tile([P, 512], F32, name="acc", tag="acc", bufs=4)
-                acc2[(hc, tt, which)] = a
-                u = hc * 2 + which
-                for gl in range(4):
-                    nc.tensor.matmul_mx(
-                        out=a[:],
-                        lhsT=qc[gl][:, tt * P:(tt + 1) * P].bitcast(FP8X4),
-                        lhsT_scale=qp[4 * gl:P, tt * P:(tt + 1) * P],
-                        rhs=uc[u][:, gl * 512:(gl + 1) * 512].bitcast(FP8X4),
-                        rhs_scale=up[u][4 * gl:P, :],
-                        start=(gl == 0),
-                        stop=(gl == 3),
-                    )
+        def stage2_passes(hc, tt, which):
+            a = ps.tile([P, 512], F32, name="acc", tag="acc", bufs=4)
+            acc2[(hc, tt, which)] = a
+            unit = hc * 2 + which
+            for gl in range(4):
+                nc.tensor.matmul_mx(
+                    out=a[:],
+                    lhsT=qc[gl][:, tt * P:(tt + 1) * P].bitcast(FP8X4),
+                    lhsT_scale=qp[4 * gl:P, tt * P:(tt + 1) * P],
+                    rhs=uc[unit][:, gl * 512:(gl + 1) * 512].bitcast(FP8X4),
+                    rhs_scale=up[unit][4 * gl:P, :],
+                    start=(gl == 0),
+                    stop=(gl == 3),
+                )
 
         def heads(ap, n):
             return ap.rearrange("p (h d) -> p h d", h=n)
@@ -250,62 +247,66 @@ def tile_multiheadlatentattention_pa_l_kernel(tc, x, Wq_d, bq_d, Wq_u, bq_u, Wrq
         def table(col, width, n):
             return trig[:, col:col + width].unsqueeze(1).to_broadcast([P, n, width])
 
-        def epi_bias(hc, tt, half, which):
-            key = (hc, tt - 4 * half)
+        def add_bias(hc, tt, half, which):
+            pair = (hc, tt - 4 * half)
             if which == 1:
                 if half == 0:
-                    tuv[key] = slot([P, 2048], F32, "tv")
+                    tv[pair] = slot([P, 2048], F32, "tv")
                 nc.vector.tensor_tensor(
-                    out=tuv[key][:, half * 512:(half + 1) * 512],
+                    out=tv[pair][:, half * 512:(half + 1) * 512],
                     in0=acc2[(hc, tt, 1)][:],
                     in1=bias2[1][:, hc * 512:(hc + 1) * 512],
                     op=ALU.add,
                 )
             else:
                 if half == 0:
-                    otile[key] = slot([P, 2048], F32, "o")
+                    o[pair] = slot([P, 2048], F32, "o")
                 nc.vector.tensor_tensor(
-                    out=heads(otile[key][:, half * 1024:(half + 1) * 1024], 8)[:, :, 0:64],
+                    out=heads(o[pair][:, half * 1024:(half + 1) * 1024], 8)[:, :, 0:64],
                     in0=heads(acc2[(hc, tt, 0)][:], 8),
                     in1=heads(bias2[0][:, hc * 512:(hc + 1) * 512], 8),
                     op=ALU.add,
                 )
 
-        def epi_sin(key):
-            a = key[1] % 4
-            t3 = heads(tuv[key][:, 0:1024], 16)
-            v3 = heads(tuv[key][:, 1024:2048], 16)
+        def sine_products(pair):
+            a = pair[1] % 4
+            t3 = heads(tv[pair][:, 0:1024], 16)
+            v3 = heads(tv[pair][:, 1024:2048], 16)
             nc.vector.tensor_tensor(out=v3[:, :, 0:32], in0=t3[:, :, 32:64], in1=table(256 + a * 64, 32, 16), op=ALU.mult)
             nc.vector.tensor_tensor(out=v3[:, :, 32:64], in0=t3[:, :, 0:32], in1=table(256 + a * 64 + 32, 32, 16), op=ALU.mult)
 
-        def epi_cos(key):
-            a = key[1] % 4
-            gh = GH
+        def cosine_products(pair):
+            a = pair[1] % 4
+            gh = GPSIMD_HEADS
             u = sb.tile([P, 1024], F32, name="u", tag="u", bufs=1, align_bytes=64)
-            utile[key] = u
-            t3 = heads(tuv[key][:, 0:1024], 16)
+            cosp[pair] = u
+            t3 = heads(tv[pair][:, 0:1024], 16)
             u3 = heads(u[:], 16)
             nc.vector.tensor_tensor(out=u3[:, gh:16, :], in0=t3[:, gh:16, :], in1=table(a * 64, 64, 16 - gh), op=ALU.mult)
-            if gh > 0:
-                nc.gpsimd.tensor_tensor(out=u3[:, 0:gh, :], in0=t3[:, 0:gh, :], in1=table(a * 64, 64, gh), op=ALU.mult)
+            nc.gpsimd.tensor_tensor(out=u3[:, 0:gh, :], in0=t3[:, 0:gh, :], in1=table(a * 64, 64, gh), op=ALU.mult)
 
-        def epi_sum(key):
-            hc, tt = key
-            o = otile[key]
+        def sum_and_store(pair):
+            hc, tt = pair
             nc.vector.tensor_tensor(
-                out=heads(o[:], 16)[:, :, 64:128],
-                in0=heads(utile[key][:], 16),
-                in1=heads(tuv[key][:, 1024:2048], 16),
+                out=heads(o[pair][:], 16)[:, :, 64:128],
+                in0=heads(cosp[pair][:], 16),
+                in1=heads(tv[pair][:, 1024:2048], 16),
                 op=ALU.add,
             )
             for half in (0, 1):
                 t0 = (tt + 4 * half) * P
                 nc.sync.dma_start(
                     out=out_flat[t0:t0 + P, hc * 1024:(hc + 1) * 1024],
-                    in_=o[:, half * 1024:(half + 1) * 1024],
+                    in_=o[pair][:, half * 1024:(half + 1) * 1024],
                 )
 
-        def rope_tables():
+        def load_stage2_biases():
+            for which, b in ((0, bq_u), (1, brq)):
+                t = slot([P, 4096], BF16, "bias2")
+                bias2[which] = t
+                nc.sync.dma_start(out=t[:], in_=b.partition_broadcast(P))
+
+        def build_rope_tables():
             scr = slot([P, 2048], F32, "scr")
 
             def reg(n):
@@ -316,112 +317,107 @@ def tile_multiheadlatentattention_pa_l_kernel(tc, x, Wq_d, bq_d, Wq_u, bq_u, Wrq
             pos_f = scr[:, 0:4]
             nc.gpsimd.iota(pos_i[:], pattern=[[P, 4]], base=0, channel_multiplier=1)
             nc.vector.tensor_copy(out=pos_f, in_=pos_i[:])
-            tr = reg(1)
-            tr4 = tr.rearrange("p (s a j) -> p s a j", s=2, a=4)
+            turns = reg(1)
+            turns4 = turns.rearrange("p (s a j) -> p s a j", s=2, a=4)
             for j in range(32):
                 nc.vector.tensor_scalar(
-                    out=tr4[:, 0, :, j], in0=pos_f,
+                    out=turns4[:, 0, :, j], in0=pos_f,
                     scalar1=10000.0 ** (-j / 32.0) / (2.0 * PI), scalar2=None, op0=ALU.mult,
                 )
-            nc.vector.tensor_scalar(out=tr4[:, 1, :, :], in0=tr4[:, 0, :, :], scalar1=0.25, scalar2=None, op0=ALU.add)
-            nc.vector.tensor_copy(out=n_i[:], in_=tr)
-            nf = reg(3)
-            nc.vector.tensor_copy(out=nf, in_=n_i[:])
+            nc.vector.tensor_scalar(out=turns4[:, 1, :, :], in0=turns4[:, 0, :, :], scalar1=0.25, scalar2=None, op0=ALU.add)
+            nc.vector.tensor_copy(out=n_i[:], in_=turns)
+            whole = reg(3)
+            nc.vector.tensor_copy(out=whole, in_=n_i[:])
             f0 = reg(4)
-            nc.vector.tensor_tensor(out=f0, in0=tr, in1=nf, op=ALU.subtract)
-            m = reg(5)
-            nc.vector.tensor_single_scalar(out=m, in_=f0, scalar=0.5, op=ALU.is_gt)
+            nc.vector.tensor_tensor(out=f0, in0=turns, in1=whole, op=ALU.subtract)
+            over = reg(5)
+            nc.vector.tensor_single_scalar(out=over, in_=f0, scalar=0.5, op=ALU.is_gt)
             f1 = reg(6)
-            nc.vector.tensor_tensor(out=f1, in0=f0, in1=m, op=ALU.subtract)
-            a1 = reg(7)
-            nc.vector.tensor_scalar(out=a1, in0=f1, scalar1=-1.0, scalar2=0.5, op0=ALU.mult, op1=ALU.add)
-            g1 = reg(2)
-            nc.vector.tensor_tensor(out=g1, in0=f1, in1=a1, op=ALU.min)
-            a2 = reg(3)
-            nc.vector.tensor_scalar(out=a2, in0=f1, scalar1=-1.0, scalar2=-0.5, op0=ALU.mult, op1=ALU.add)
-            g2 = reg(4)
-            nc.vector.tensor_tensor(out=g2, in0=g1, in1=a2, op=ALU.max)
-            g4 = g2.rearrange("p (s a j) -> p s a j", s=2, a=4)
-            cb = trig[:, 0:256].rearrange("p (a f j) -> p a f j", a=4, f=2)
-            sn = trig[:, 256:512].rearrange("p (a f j) -> p a f j", a=4, f=2)
+            nc.vector.tensor_tensor(out=f1, in0=f0, in1=over, op=ALU.subtract)
+            up_fold = reg(7)
+            nc.vector.tensor_scalar(out=up_fold, in0=f1, scalar1=-1.0, scalar2=0.5, op0=ALU.mult, op1=ALU.add)
+            f2 = reg(2)
+            nc.vector.tensor_tensor(out=f2, in0=f1, in1=up_fold, op=ALU.min)
+            down_fold = reg(3)
+            nc.vector.tensor_scalar(out=down_fold, in0=f1, scalar1=-1.0, scalar2=-0.5, op0=ALU.mult, op1=ALU.add)
+            f3 = reg(4)
+            nc.vector.tensor_tensor(out=f3, in0=f2, in1=down_fold, op=ALU.max)
+            f4 = f3.rearrange("p (s a j) -> p s a j", s=2, a=4)
+            cos_t = trig[:, 0:256].rearrange("p (a f j) -> p a f j", a=4, f=2)
+            sin_t = trig[:, 256:512].rearrange("p (a f j) -> p a f j", a=4, f=2)
             two_pi = 2.0 * PI
-            nc.scalar.activation(out=sn[:, :, 0, :], in_=g4[:, 0, :, :], func=ACT.Sin, scale=-two_pi)
-            nc.scalar.activation(out=sn[:, :, 1, :], in_=g4[:, 0, :, :], func=ACT.Sin, scale=two_pi)
-            nc.scalar.activation(out=cb[:, :, 0, :], in_=g4[:, 1, :, :], func=ACT.Sin, scale=two_pi)
-            nc.scalar.activation(out=cb[:, :, 1, :], in_=g4[:, 1, :, :], func=ACT.Sin, scale=two_pi)
+            nc.scalar.activation(out=sin_t[:, :, 0, :], in_=f4[:, 0, :, :], func=ACT.Sin, scale=-two_pi)
+            nc.scalar.activation(out=sin_t[:, :, 1, :], in_=f4[:, 0, :, :], func=ACT.Sin, scale=two_pi)
+            nc.scalar.activation(out=cos_t[:, :, 0, :], in_=f4[:, 1, :, :], func=ACT.Sin, scale=two_pi)
+            nc.scalar.activation(out=cos_t[:, :, 1, :], in_=f4[:, 1, :, :], func=ACT.Sin, scale=two_pi)
 
-        def load_bias2():
-            for which, b in ((0, bq_u), (1, brq)):
-                t = slot([P, 4096], BF16, "bias2")
-                bias2[which] = t
-                nc.sync.dma_start(out=t[:], in_=b.partition_broadcast(P))
-
-        prog = []
-        where = {}
-        for i in range(NRUN):
-            where[runs[i]] = i
-        todo = []
+        steps = []
+        pieces = []
         for c in range(4):
             for hf in (0, 1):
-                for grp in range(KH):
+                for grp in range(HEAD_GROUPS):
                     for j in (2 * hf, 2 * hf + 1):
-                        need = max(where[("wd", grp, hf)], where[("x", 2 * c + 1, j)])
-                        todo.append((grp, c, 4 * j, 4 * j + 4, need))
-        for grp in range(KH, 16):
+                        need = max(index_of[("wd", grp, hf)], index_of[("x", 2 * c + 1, j)])
+                        pieces.append((grp, c, 4 * j, 4 * j + 4, need))
+        for grp in range(HEAD_GROUPS, 16):
             for c in range(4):
-                todo.append((grp, c, 0, 16, 0))
-        done = [0, 0]
+                pieces.append((grp, c, 0, 16, 0))
+        taken = [0, 0]
 
-        def take(limit, ready, upto):
+        def take_piece(n_passes):
+            grp, c, g0, g1, need = pieces[taken[0]]
+            ga = g0 + taken[1]
+            gb = min(g1, ga + n_passes)
+            steps.append(("M1", grp, c, ga, gb))
+            if gb == g1:
+                taken[0] += 1
+                taken[1] = 0
+            else:
+                taken[1] = gb - g0
+            return gb - ga
+
+        def take_ready(run):
             n = 0
-            while done[0] < len(todo):
-                grp, c, g0, g1, need = todo[done[0]]
-                if upto is not None and (grp, c) > upto:
-                    break
-                if upto is None and (need > ready or n >= limit):
-                    break
-                ga = g0 + done[1]
-                gb = g1 if upto is not None else min(g1, ga + limit - n)
-                prog.append(("M1", grp, c, ga, gb))
-                n += gb - ga
-                if gb == g1:
-                    done[0] += 1
-                    done[1] = 0
-                else:
-                    done[1] = gb - g0
+            while taken[0] < len(pieces) and pieces[taken[0]][4] <= run - READY_LAG and n < HEAD_PASSES:
+                n += take_piece(HEAD_PASSES - n)
 
-        for i in range(NHEAD):
-            prog.append(("T", i))
-            take(MAXP, i - LAG, None)
-        nxt = NHEAD
-        for grp in range(KH, 16):
+        def take_through(grp, c):
+            while taken[0] < len(pieces) and pieces[taken[0]][0:2] <= (grp, c):
+                take_piece(16)
+
+        for i in range(n_head):
+            steps.append(("T", i))
+            take_ready(i)
+        run = n_head
+        for grp in range(HEAD_GROUPS, 16):
             for hf in (0, 1):
-                prog.append(("T", nxt))
-                nxt += 1
-                take(0, 0, (grp - 1, 2 * hf + 1))
-                if (grp, hf) == ROPE_AT:
-                    prog.append(("ROPE",))
+                steps.append(("T", run))
+                run += 1
+                take_through(grp - 1, 2 * hf + 1)
+                if (grp, hf) == ROPE_AFTER:
+                    steps.append(("ROPE",))
         for c in range(4):
-            prog.append(("T", nxt))
-            nxt += 1
-            take(0, 0, (15, c))
+            steps.append(("T", run))
+            run += 1
+            take_through(15, c)
             if c == 1:
-                prog.append(("B2",))
+                steps.append(("B2",))
+        first_run_in_stage2 = run
         for hc in range(8):
-            for qd in range(4):
+            for quarter in range(4):
                 if hc < 7:
-                    prog.append(("T", nxt))
-                    nxt += 1
-                for tt in TT_FIRST[2 * qd:2 * qd + 2]:
-                    prog.append(("M2", hc, tt))
-        assert nxt == NRUN
+                    steps.append(("T", run))
+                    run += 1
+                for tt in PAIR_FIRST[2 * quarter:2 * quarter + 2]:
+                    steps.append(("M2", hc, tt))
+        assert run == n_runs
 
         later = []
 
-        def defer(n, fn):
+        def after(n, fn):
             later.append([n + 1, fn])
 
-        def tick():
+        def step_done():
             due = []
             keep = []
             for e in later:
@@ -435,64 +431,65 @@ def tile_multiheadlatentattention_pa_l_kernel(tc, x, Wq_d, bq_d, Wq_u, bq_u, Wrq
                 e[1]()
 
         loaded = [0]
-        pend = []
-        wq = []
 
-        def load_upto(n):
-            while loaded[0] < min(n, NRUN):
-                load(loaded[0])
+        def load_runs_before(n):
+            while loaded[0] < min(n, n_runs):
+                load_run(loaded[0])
                 loaded[0] += 1
 
-        load_upto(LD_HEAD)
+        unsummed = []
+        unquantized = []
+
+        load_runs_before(LOAD_AHEAD_HEAD)
         nc.sync.dma_start(
             out=bqd_sb[:].rearrange("p (g t) -> p g t", g=4),
             in_=bq_d.rearrange("(g m t) -> m g t", g=4, t=4),
         )
-        sort(0, 0)
+        sort_run(0)
 
-        for item in prog:
-            if item[0] == "T":
-                i = item[1]
-                transp(i)
-                copyout(i)
-                if i + 1 < NRUN:
-                    load_upto(i + 2)
-                    sort(i + 1, 8 if runs[i + 1][0] == "w2" else (SSH if i + 1 < NHEAD else 0))
-                load_upto(i + 1 + (LD_HEAD if i < NHEAD - 2 else LD_STEADY))
-                if i >= NRUN - 28:
-                    wq.append(i)
+        for step in steps:
+            if step[0] == "T":
+                i = step[1]
+                transpose_run(i)
+                copy_out_run(i)
+                if i + 1 < n_runs:
+                    load_runs_before(i + 2)
+                    sort_run(i + 1)
+                load_runs_before(i + 1 + (LOAD_AHEAD_HEAD if i < n_head - 2 else LOAD_AHEAD))
+                if i >= first_run_in_stage2:
+                    unquantized.append(i)
                 else:
-                    defer(QLAG, lambda i=i: quant(i))
-            elif item[0] == "M1":
-                grp, c, g0, g1 = item[1], item[2], item[3], item[4]
-                mm1(grp, c, g0, g1)
+                    after(1, lambda i=i: quantize_run(i))
+            elif step[0] == "M1":
+                grp, c, g0, g1 = step[1], step[2], step[3], step[4]
+                stage1_passes(grp, c, g0, g1)
                 if g1 == 16:
-                    evac1(grp, c)
+                    stage1_bias(grp, c)
                     if grp % 4 == 3:
-                        defer(1, lambda c=c: weave_q(c))
-                        defer(2, lambda gl=grp // 4, c=c: quant_q(gl, c))
+                        after(1, lambda c=c: interleave_q(c))
+                        after(2, lambda gl=grp // 4, c=c: quantize_q(gl, c))
                     if (grp, c) == (15, 3):
                         while len(later) > 0:
-                            tick()
-            elif item[0] == "B2":
-                load_bias2()
-            elif item[0] == "ROPE":
-                rope_tables()
+                            step_done()
+            elif step[0] == "B2":
+                load_stage2_biases()
+            elif step[0] == "ROPE":
+                build_rope_tables()
             else:
-                hc, tt = item[1], item[2]
-                key = (hc, tt)
+                hc, tt = step[1], step[2]
+                pair = (hc, tt)
                 for which in (1, 0):
                     for half in (0, 1):
-                        mm2(hc, tt + 4 * half, which)
-                        epi_bias(hc, tt + 4 * half, half, which)
-                epi_sin(key)
-                while len(wq) > 0:
-                    quant(wq.pop(0))
-                if len(pend) > 0:
-                    epi_sum(pend.pop(0))
-                epi_cos(key)
-                pend.append(key)
-            tick()
+                        stage2_passes(hc, tt + 4 * half, which)
+                        add_bias(hc, tt + 4 * half, half, which)
+                sine_products(pair)
+                while len(unquantized) > 0:
+                    quantize_run(unquantized.pop(0))
+                if len(unsummed) > 0:
+                    sum_and_store(unsummed.pop(0))
+                cosine_products(pair)
+                unsummed.append(pair)
+            step_done()
         while len(later) > 0:
-            tick()
-        epi_sum(pend.pop(0))
+            step_done()
+        sum_and_store(unsummed.pop(0))

from contextlib import ExitStack

import concourse.mybir as mybir
from concourse.masks import make_identity

FLOPS = 2 * 2048 * 8192 * 2048 * 2

F32 = mybir.dt.float32
BF16 = mybir.dt.bfloat16
U32 = mybir.dt.uint32
I32 = mybir.dt.int32
U8 = mybir.dt.uint8
FP8X4 = mybir.dt.float8_e4m3fn_x4
ALU = mybir.AluOpType
ACT = mybir.ActivationFunctionType

P = 128
PI = 3.141592653589793

SLOTS = 25
HEAD_GROUPS = 3
HEAD_PASSES = 8
READY_LAG = 2
LOAD_AHEAD_HEAD = 3
LOAD_AHEAD = 2
ROPE_AFTER = (5, 0)
PAIR_FIRST = (0, 1, 2, 3, 8, 9, 10, 11)
GPSIMD_HEADS = 12


def tile_multiheadlatentattention_pa_l_kernel(tc, x, Wq_d, bq_d, Wq_u, bq_u, Wrq, brq, out):
    nc = tc.nc
    x_flat = x.flatten_outer_dims()
    out_flat = out.rearrange("b s h d -> (b s) (h d)")
    wd_groups = Wq_d.rearrange("(g m t) k -> g t m k", g=4, t=4)

    with ExitStack() as ctx:
        ctx.enter_context(tc.manual_schedule())
        sb = ctx.enter_context(tc.tile_pool(name="sb", bufs=1))
        ps = ctx.enter_context(tc.psum_pool(name="ps", bufs=4))

        def slot(shape, dtype, name):
            return sb.tile(shape, dtype, name=name, tag="slot", bufs=SLOTS, align_bytes=64)

        ident = sb.tile([P, P], F32, name="ident")
        make_identity(nc, ident[:])
        bqd_sb = sb.tile([P, 16], BF16, name="bqd_sb")
        trig = sb.tile([P, 512], F32, name="trig")
        qp = sb.tile([P, 2048], U8, name="qp", align_bytes=64)

        runs = []
        for hf in (0, 1):
            runs.append(("wd", 0, hf))
            for kq in (2 * hf, 2 * hf + 1):
                for rp in (0, 1):
                    runs.append(("x", rp, kq))
            for grp in range(1, HEAD_GROUPS):
                runs.append(("wd", grp, hf))
        for c in (1, 2, 3):
            for kq in range(4):
                for rp in (0, 1):
                    runs.append(("x", 2 * c + rp, kq))
        n_head = len(runs)
        for grp in range(HEAD_GROUPS, 16):
            for hf in (0, 1):
                runs.append(("wd", grp, hf))
        for unit in range(16):
            for rp in (0, 1):
                runs.append(("w2", unit, rp))
        n_runs = len(runs)
        index_of = {}
        for i in range(n_runs):
            index_of[runs[i]] = i

        raw = {}
        srt = {}
        tps = {}
        grpd = {}
        wc, wp = {}, {}
        xc, xp = {}, {}
        uc, up = {}, {}

        def load_run(i):
            kind, a, b = runs[i]
            r = slot([P, 4096], BF16, "raw")
            raw[i] = r
            if kind == "wd":
                nc.sync.dma_start(out=r[:], in_=wd_groups[a // 4, a % 4][:, b * 4096:(b + 1) * 4096])
            else:
                if kind == "x":
                    rows = x_flat[a * 256:(a + 1) * 256, b * 2048:(b + 1) * 2048]
                else:
                    w = Wq_u if a % 2 == 0 else Wrq
                    r0 = (a // 2) * 512 + b * 256
                    rows = w[r0:r0 + 256, :]
                nc.sync.dma_start(
                    out=r[:].rearrange("p (r k) -> p r k", r=2),
                    in_=rows.rearrange("(r p) k -> p r k", p=P),
                )

        def sort_run(i):
            s = slot([P, 2048], F32, "srt")
            srt[i] = s
            dst = s[:].rearrange("p (b u q) -> p b u q", b=8, u=2)
            src = raw[i][:].bitcast(F32).rearrange("p (b q u) -> p b u q", b=8, u=2)
            if runs[i][0] == "w2":
                nc.scalar.copy(out=dst[:, 0:8], in_=src[:, 0:8])
            else:
                nc.vector.tensor_copy(out=dst[:, 0:8], in_=src[:, 0:8])

        def transpose_run(i):
            banks = []
            for k in range(4):
                t = ps.tile([P, 4, P], F32, name="tp", tag="tp", bufs=4)
                banks.append(t)
                for s in range(4):
                    c0 = (k * 4 + s) * P
                    nc.tensor.transpose(out=t[:, s, :], in_=srt[i][:, c0:c0 + P], identity=ident[:])
            tps[i] = banks

        def copy_out_run(i):
            g = slot([P, 4096], BF16, "grpd")
            grpd[i] = g
            gw = g[:].bitcast(F32)
            for k in range(4):
                if runs[i][0] == "wd":
                    dst = gw[:, k * 512:(k + 1) * 512].rearrange("p (b r u) -> p b r u", b=2, u=2)
                else:
                    g0 = 2 * (k % 2)
                    dst = gw.rearrange("p (g r w) -> p g r w", g=4, r=2)[:, g0:g0 + 2, k // 2, :]
                    dst = dst.rearrange("p b (r u) -> p b r u", u=2)
                nc.scalar.copy(out=dst, in_=tps[i][k][:].rearrange("p (b u) r -> p b r u", u=2))

        def quantize_run(i):
            kind, a, b = runs[i]
            g = grpd[i]
            if kind == "wd":
                if b == 0:
                    wc[a] = slot([P, 2048], U32, "wc")
                    wp[a] = sb.tile([P, 512], U8, name="wp", tag="wp", bufs=4, align_bytes=64)
                for j2 in (0, 1):
                    j = b * 2 + j2
                    nc.vector.quantize_mx(
                        out=wc[a][:, j * 512:(j + 1) * 512].bitcast(FP8X4),
                        scales=wp[a][4 * j:P, :],
                        in_=g[:, j2 * 2048:(j2 + 1) * 2048],
                    )
            else:
                if kind == "x":
                    c, rp, j = a // 2, a % 2, b
                    if rp == 0 and j == 0:
                        xp[c] = sb.tile([P, 2048], U8, name="xp", tag="xp", bufs=4, align_bytes=64)
                    if rp == 0:
                        xc[(c, j)] = slot([P, 2048], U32, "xc")
                    codes, plane = xc[(c, j)], xp[c]
                else:
                    rp = b
                    if rp == 0:
                        uc[a] = slot([P, 2048], U32, "uc")
                        up[a] = sb.tile([P, 512], U8, name="up", tag="wp", bufs=4, align_bytes=64)
                    codes, plane = uc[a], up[a]
                for gl in range(4):
                    c0 = gl * 512 + rp * 256
                    if kind == "x":
                        sc = plane[4 * j:P, c0:c0 + 256]
                    else:
                        sc = plane[4 * gl:P, rp * 256:rp * 256 + 256]
                    nc.vector.quantize_mx(
                        out=codes[:, c0:c0 + 256].bitcast(FP8X4),
                        scales=sc,
                        in_=g[:, gl * 1024:(gl + 1) * 1024],
                    )

        acc1 = {}
        qg = {}
        qi = {}
        qc = {}

        def stage1_passes(grp, c, g0, g1):
            if g0 == 0:
                acc1[(grp, c)] = ps.tile([P, 512], F32, name="acc", tag="acc", bufs=4)
            a = acc1[(grp, c)]
            for gp in range(g0, g1):
                j = gp // 4
                nc.tensor.matmul_mx(
                    out=a[:],
                    lhsT=wc[grp][:, gp * P:(gp + 1) * P].bitcast(FP8X4),
                    lhsT_scale=wp[grp][4 * j:P, (gp % 4) * P:(gp % 4 + 1) * P],
                    rhs=xc[(c, j)][:, (gp % 4) * 512:(gp % 4 + 1) * 512].bitcast(FP8X4),
                    rhs_scale=xp[c][4 * j:P, (gp % 4) * 512:(gp % 4 + 1) * 512],
                    start=(gp == 0),
                    stop=(gp == 15),
                )

        def stage1_bias(grp, c):
            t = grp % 4
            if t == 0:
                qg[c] = sb.tile([P, 2048], BF16, name="qg", tag="qg", bufs=4, align_bytes=64)
            nc.scalar.activation(
                out=qg[c][:, t * 512:(t + 1) * 512],
                in_=acc1[(grp, c)][:],
                func=ACT.Identity,
                bias=bqd_sb[:, grp:grp + 1],
                scale=1.0,
            )

        def interleave_q(c):
            qi[c] = sb.tile([P, 2048], BF16, name="qi", tag="u", bufs=1, align_bytes=64)
            nc.vector.tensor_copy(
                out=qi[c][:].rearrange("p (n t) -> p n t", t=4),
                in_=qg[c][:].rearrange("p (t n) -> p n t", t=4),
            )

        def quantize_q(gl, c):
            if c == 0:
                qc[gl] = slot([P, 2048], U32, "qc")
            nc.vector.quantize_mx(
                out=qc[gl][:, c * 512:(c + 1) * 512].bitcast(FP8X4),
                scales=qp[4 * gl:P, c * 512:(c + 1) * 512],
                in_=qi[c][:],
            )

        acc2 = {}
        bias2 = {}
        tv = {}
        cosp = {}
        o = {}

        def stage2_passes(hc, tt, which):
            a = ps.tile([P, 512], F32, name="acc", tag="acc", bufs=4)
            acc2[(hc, tt, which)] = a
            unit = hc * 2 + which
            for gl in range(4):
                nc.tensor.matmul_mx(
                    out=a[:],
                    lhsT=qc[gl][:, tt * P:(tt + 1) * P].bitcast(FP8X4),
                    lhsT_scale=qp[4 * gl:P, tt * P:(tt + 1) * P],
                    rhs=uc[unit][:, gl * 512:(gl + 1) * 512].bitcast(FP8X4),
                    rhs_scale=up[unit][4 * gl:P, :],
                    start=(gl == 0),
                    stop=(gl == 3),
                )

        def heads(ap, n):
            return ap.rearrange("p (h d) -> p h d", h=n)

        def table(col, width, n):
            return trig[:, col:col + width].unsqueeze(1).to_broadcast([P, n, width])

        def add_bias(hc, tt, half, which):
            pair = (hc, tt - 4 * half)
            if which == 1:
                if half == 0:
                    tv[pair] = slot([P, 2048], F32, "tv")
                nc.vector.tensor_tensor(
                    out=tv[pair][:, half * 512:(half + 1) * 512],
                    in0=acc2[(hc, tt, 1)][:],
                    in1=bias2[1][:, hc * 512:(hc + 1) * 512],
                    op=ALU.add,
                )
            else:
                if half == 0:
                    o[pair] = slot([P, 2048], F32, "o")
                nc.vector.tensor_tensor(
                    out=heads(o[pair][:, half * 1024:(half + 1) * 1024], 8)[:, :, 0:64],
                    in0=heads(acc2[(hc, tt, 0)][:], 8),
                    in1=heads(bias2[0][:, hc * 512:(hc + 1) * 512], 8),
                    op=ALU.add,
                )

        def sine_products(pair):
            a = pair[1] % 4
            t3 = heads(tv[pair][:, 0:1024], 16)
            v3 = heads(tv[pair][:, 1024:2048], 16)
            nc.vector.tensor_tensor(out=v3[:, :, 0:32], in0=t3[:, :, 32:64], in1=table(256 + a * 64, 32, 16), op=ALU.mult)
            nc.vector.tensor_tensor(out=v3[:, :, 32:64], in0=t3[:, :, 0:32], in1=table(256 + a * 64 + 32, 32, 16), op=ALU.mult)

        def cosine_products(pair):
            a = pair[1] % 4
            gh = GPSIMD_HEADS
            u = sb.tile([P, 1024], F32, name="u", tag="u", bufs=1, align_bytes=64)
            cosp[pair] = u
            t3 = heads(tv[pair][:, 0:1024], 16)
            u3 = heads(u[:], 16)
            nc.vector.tensor_tensor(out=u3[:, gh:16, :], in0=t3[:, gh:16, :], in1=table(a * 64, 64, 16 - gh), op=ALU.mult)
            nc.gpsimd.tensor_tensor(out=u3[:, 0:gh, :], in0=t3[:, 0:gh, :], in1=table(a * 64, 64, gh), op=ALU.mult)

        def sum_and_store(pair):
            hc, tt = pair
            nc.vector.tensor_tensor(
                out=heads(o[pair][:], 16)[:, :, 64:128],
                in0=heads(cosp[pair][:], 16),
                in1=heads(tv[pair][:, 1024:2048], 16),
                op=ALU.add,
            )
            for half in (0, 1):
                t0 = (tt + 4 * half) * P
                nc.sync.dma_start(
                    out=out_flat[t0:t0 + P, hc * 1024:(hc + 1) * 1024],
                    in_=o[pair][:, half * 1024:(half + 1) * 1024],
                )

        def load_stage2_biases():
            for which, b in ((0, bq_u), (1, brq)):
                t = slot([P, 4096], BF16, "bias2")
                bias2[which] = t
                nc.sync.dma_start(out=t[:], in_=b.partition_broadcast(P))

        def build_rope_tables():
            scr = slot([P, 2048], F32, "scr")

            def reg(n):
                return scr[:, 256 * n:256 * (n + 1)]

            pos_i = sb.tile([P, 4], I32, name="pos_i")
            n_i = sb.tile([P, 256], I32, name="n_i")
            pos_f = scr[:, 0:4]
            nc.gpsimd.iota(pos_i[:], pattern=[[P, 4]], base=0, channel_multiplier=1)
            nc.vector.tensor_copy(out=pos_f, in_=pos_i[:])
            turns = reg(1)
            turns4 = turns.rearrange("p (s a j) -> p s a j", s=2, a=4)
            for j in range(32):
                nc.vector.tensor_scalar(
                    out=turns4[:, 0, :, j], in0=pos_f,
                    scalar1=10000.0 ** (-j / 32.0) / (2.0 * PI), scalar2=None, op0=ALU.mult,
                )
            nc.vector.tensor_scalar(out=turns4[:, 1, :, :], in0=turns4[:, 0, :, :], scalar1=0.25, scalar2=None, op0=ALU.add)
            nc.vector.tensor_copy(out=n_i[:], in_=turns)
            whole = reg(3)
            nc.vector.tensor_copy(out=whole, in_=n_i[:])
            f0 = reg(4)
            nc.vector.tensor_tensor(out=f0, in0=turns, in1=whole, op=ALU.subtract)
            over = reg(5)
            nc.vector.tensor_single_scalar(out=over, in_=f0, scalar=0.5, op=ALU.is_gt)
            f1 = reg(6)
            nc.vector.tensor_tensor(out=f1, in0=f0, in1=over, op=ALU.subtract)
            up_fold = reg(7)
            nc.vector.tensor_scalar(out=up_fold, in0=f1, scalar1=-1.0, scalar2=0.5, op0=ALU.mult, op1=ALU.add)
            f2 = reg(2)
            nc.vector.tensor_tensor(out=f2, in0=f1, in1=up_fold, op=ALU.min)
            down_fold = reg(3)
            nc.vector.tensor_scalar(out=down_fold, in0=f1, scalar1=-1.0, scalar2=-0.5, op0=ALU.mult, op1=ALU.add)
            f3 = reg(4)
            nc.vector.tensor_tensor(out=f3, in0=f2, in1=down_fold, op=ALU.max)
            f4 = f3.rearrange("p (s a j) -> p s a j", s=2, a=4)
            cos_t = trig[:, 0:256].rearrange("p (a f j) -> p a f j", a=4, f=2)
            sin_t = trig[:, 256:512].rearrange("p (a f j) -> p a f j", a=4, f=2)
            two_pi = 2.0 * PI
            nc.scalar.activation(out=sin_t[:, :, 0, :], in_=f4[:, 0, :, :], func=ACT.Sin, scale=-two_pi)
            nc.scalar.activation(out=sin_t[:, :, 1, :], in_=f4[:, 0, :, :], func=ACT.Sin, scale=two_pi)
            nc.scalar.activation(out=cos_t[:, :, 0, :], in_=f4[:, 1, :, :], func=ACT.Sin, scale=two_pi)
            nc.scalar.activation(out=cos_t[:, :, 1, :], in_=f4[:, 1, :, :], func=ACT.Sin, scale=two_pi)

        steps = []
        pieces = []
        for c in range(4):
            for hf in (0, 1):
                for grp in range(HEAD_GROUPS):
                    for j in (2 * hf, 2 * hf + 1):
                        need = max(index_of[("wd", grp, hf)], index_of[("x", 2 * c + 1, j)])
                        pieces.append((grp, c, 4 * j, 4 * j + 4, need))
        for grp in range(HEAD_GROUPS, 16):
            for c in range(4):
                pieces.append((grp, c, 0, 16, 0))
        taken = [0, 0]

        def take_piece(n_passes):
            grp, c, g0, g1, need = pieces[taken[0]]
            ga = g0 + taken[1]
            gb = min(g1, ga + n_passes)
            steps.append(("M1", grp, c, ga, gb))
            if gb == g1:
                taken[0] += 1
                taken[1] = 0
            else:
                taken[1] = gb - g0
            return gb - ga

        def take_ready(run):
            n = 0
            while taken[0] < len(pieces) and pieces[taken[0]][4] <= run - READY_LAG and n < HEAD_PASSES:
                n += take_piece(HEAD_PASSES - n)

        def take_through(grp, c):
            while taken[0] < len(pieces) and pieces[taken[0]][0:2] <= (grp, c):
                take_piece(16)

        for i in range(n_head):
            steps.append(("T", i))
            take_ready(i)
        run = n_head
        for grp in range(HEAD_GROUPS, 16):
            for hf in (0, 1):
                steps.append(("T", run))
                run += 1
                take_through(grp - 1, 2 * hf + 1)
                if (grp, hf) == ROPE_AFTER:
                    steps.append(("ROPE",))
        for c in range(4):
            steps.append(("T", run))
            run += 1
            take_through(15, c)
            if c == 1:
                steps.append(("B2",))
        first_run_in_stage2 = run
        for hc in range(8):
            for quarter in range(4):
                if hc < 7:
                    steps.append(("T", run))
                    run += 1
                for tt in PAIR_FIRST[2 * quarter:2 * quarter + 2]:
                    steps.append(("M2", hc, tt))
        assert run == n_runs

        later = []

        def after(n, fn):
            later.append([n + 1, fn])

        def step_done():
            due = []
            keep = []
            for e in later:
                e[0] -= 1
                if e[0] <= 0:
                    due.append(e)
                else:
                    keep.append(e)
            later[:] = keep
            for e in due:
                e[1]()

        loaded = [0]

        def load_runs_before(n):
            while loaded[0] < min(n, n_runs):
                load_run(loaded[0])
                loaded[0] += 1

        unsummed = []
        unquantized = []

        load_runs_before(LOAD_AHEAD_HEAD)
        nc.sync.dma_start(
            out=bqd_sb[:].rearrange("p (g t) -> p g t", g=4),
            in_=bq_d.rearrange("(g m t) -> m g t", g=4, t=4),
        )
        sort_run(0)

        for step in steps:
            if step[0] == "T":
                i = step[1]
                transpose_run(i)
                copy_out_run(i)
                if i + 1 < n_runs:
                    load_runs_before(i + 2)
                    sort_run(i + 1)
                load_runs_before(i + 1 + (LOAD_AHEAD_HEAD if i < n_head - 2 else LOAD_AHEAD))
                if i >= first_run_in_stage2:
                    unquantized.append(i)
                else:
                    after(1, lambda i=i: quantize_run(i))
            elif step[0] == "M1":
                grp, c, g0, g1 = step[1], step[2], step[3], step[4]
                stage1_passes(grp, c, g0, g1)
                if g1 == 16:
                    stage1_bias(grp, c)
                    if grp % 4 == 3:
                        after(1, lambda c=c: interleave_q(c))
                        after(2, lambda gl=grp // 4, c=c: quantize_q(gl, c))
                    if (grp, c) == (15, 3):
                        while len(later) > 0:
                            step_done()
            elif step[0] == "B2":
                load_stage2_biases()
            elif step[0] == "ROPE":
                build_rope_tables()
            else:
                hc, tt = step[1], step[2]
                pair = (hc, tt)
                for which in (1, 0):
                    for half in (0, 1):
                        stage2_passes(hc, tt + 4 * half, which)
                        add_bias(hc, tt + 4 * half, half, which)
                sine_products(pair)
                while len(unquantized) > 0:
                    quantize_run(unquantized.pop(0))
                if len(unsummed) > 0:
                    sum_and_store(unsummed.pop(0))
                cosine_products(pair)
                unsummed.append(pair)
            step_done()
        while len(later) > 0:
            step_done()
        sum_and_store(unsummed.pop(0))
